import numpy as np
import ml_dtypes


def mxq(x, axis, fmt="e4m3"):
    dtype, down = {"e4m3": (ml_dtypes.float8_e4m3fn, 7), "e5m2": (ml_dtypes.float8_e5m2, 14)}[fmt]
    v = np.moveaxis(np.asarray(x, np.float32).astype(ml_dtypes.bfloat16).astype(np.float64), axis, -1)
    blocks = v.reshape(v.shape[:-1] + (-1, 32))
    amax = np.abs(blocks).max(-1, keepdims=True)
    byte = np.maximum(np.where(amax > 0, np.frexp(amax)[1] - 1 + 127, 0) - down, 1)
    scale = np.exp2(byte - 127.0)
    codes = (blocks / scale).astype(np.float32).astype(dtype).astype(np.float64)
    return np.moveaxis((codes * scale).reshape(v.shape), -1, axis)


WIDE = False


def mx_kscale(k):
    if not WIDE:
        return np.ones(k)
    levels = np.array([10, -10, 5, -5, 0])
    if k % 512:
        return np.exp2(np.random.permutation(np.resize(levels, k // 32))).repeat(32)
    a = np.empty((k // 512, 16))
    for p in range(k // 512):
        a[p, :8] = np.random.permutation(np.resize(levels, 8))
        for g in range(8):
            far = levels[np.abs(levels - a[p, g]) >= 10]
            a[p, g + 8] = far[np.random.randint(len(far))]
    return np.exp2(a.ravel()).repeat(32)


BF16 = ml_dtypes.bfloat16


def bf(x):
    return np.asarray(x, np.float32).astype(BF16)


def f64(x):
    return np.asarray(x).astype(np.float64)


B, S, D, H, F = 4, 256, 1024, 16, 4096
EPS = 1e-5
NTERMS = 120


def layernorm(v, gamma, beta):
    mu = v.mean(-1, keepdims=True)
    var = np.square(v - mu).mean(-1, keepdims=True)
    return (v - mu) / np.sqrt(var + EPS) * gamma + beta


def erf(z):
    z = np.clip(z, -6.0, 6.0)
    zz = 2.0 * z * z
    term = z.copy()
    tot = z.copy()
    for n in range(1, NTERMS):
        term *= zz
        term /= 2.0 * n + 1.0
        tot += term
    return 2.0 / np.sqrt(np.pi) * np.exp(-z * z) * tot


def gelu(v):
    return 0.5 * v * (1.0 + erf(v / np.sqrt(2.0)))


def draw0():
    s, t = mx_kscale(D), mx_kscale(D)
    return {"attn_out": bf(0.25 * np.random.standard_normal((B, S, D)) * s),
            "x": bf(np.random.standard_normal((B, S, D)) * (0.5 + np.random.random((B, S, 1))) + 0.5 * np.random.standard_normal((B, S, 1))),
            "w_proj": bf(2.0 * np.random.standard_normal((D, D)) / np.sqrt(D) / s[:, None]),
            "b_proj": bf(0.1 * np.random.standard_normal(D)),
            "g2": bf((1.0 + 0.1 * np.random.standard_normal(D)) * t),
            "beta2": bf(0.1 * np.random.standard_normal(D) * t),
            "w_fc1": bf(np.random.standard_normal((D, F)) / np.sqrt(D) / t[:, None]),
            "b_fc1": bf(0.1 * np.random.standard_normal(F))}


def core(attn_out, x, w_proj, b_proj, g2, beta2, w_fc1, b_fc1):
    x_mid = f64(x) + ((mxq(f64(attn_out), 2, "e4m3") @ mxq(f64(w_proj), 0, "e4m3")) + f64(b_proj))
    h = layernorm(x_mid, f64(g2), f64(beta2))
    hid = gelu((mxq(h, 2, "e4m3") @ mxq(f64(w_fc1), 0, "e4m3")) + f64(b_fc1))
    return x_mid, hid


def e4m3fn_bytes(y):
    return np.clip(np.asarray(y, np.float64), -448.0, 448.0).astype(np.float32).astype(ml_dtypes.float8_e4m3fn).view(np.uint8)


def e4m3fn_values(b):
    return np.asarray(b, np.uint8).view(ml_dtypes.float8_e4m3fn).astype(np.float64)


def setup_inputs():
    d = draw0()
    x0 = np.asarray(d['w_fc1']).astype(np.float64)
    s = (np.max(np.abs(x0), axis=(1,), keepdims=True) / 448.0).astype(np.float32)
    out = {}
    for k, v in d.items():
        if k == 'w_fc1':
            out['w_fc1_bytes'] = e4m3fn_bytes(x0 / s.astype(np.float64))
            out['w_fc1_scale'] = s
        else:
            out[k] = v
    return out


def reference(attn_out, x, w_proj, b_proj, g2, beta2, w_fc1_bytes, w_fc1_scale, b_fc1):
    return core(attn_out, x, w_proj, b_proj, g2, beta2, e4m3fn_values(w_fc1_bytes) * w_fc1_scale.astype(np.float64), b_fc1)

@@ -1,0 +1,502 @@
+from contextlib import ExitStack
+
+import concourse.mybir as mybir
+from concourse.masks import make_identity
+
+T, D, F = 1024, 1024, 4096
+EPS = 1e-5
+FLOPS = 2 * T * D * (D + F)
+BYTES = 2 * T * D * 2 + D * D * 2 + D * F + D * 4 + (3 * D + F) * 2 + T * D * 4 + T * F * 4
+
+F32 = mybir.dt.float32
+BF16 = mybir.dt.bfloat16
+U32 = mybir.dt.uint32
+U8 = mybir.dt.uint8
+FP8 = mybir.dt.float8_e4m3fn
+FP8X4 = mybir.dt.float8_e4m3fn_x4
+ALU = mybir.AluOpType
+ACT = mybir.ActivationFunctionType
+
+P = 128
+PACK = 4
+PASSES = D // (P * PACK)
+N = 512
+TILES = T // P
+GROUP = N // P
+CHUNKS = F // N
+BLOCK = 1024
+PLANES = PASSES * PACK
+POOL_COLS = 640
+VECTOR_PLANES = 3
+
+
+def tile_flashinferblock_pb_kernel(
+    tc, attn_out, x, w_proj, b_proj, g2, beta2, w_fc1_bytes, w_fc1_scale, b_fc1, out_0, out_1
+):
+    nc = tc.nc
+    attn_rows = attn_out.rearrange("b s d -> (b s) d")
+    x_rows = x.rearrange("b s d -> (b s) d")
+    x_mid_rows = out_0.rearrange("b s d -> (b s) d")
+    hid_rows = out_1.rearrange("b s f -> (b s) f")
+    w_proj_k = w_proj.rearrange("(g p t) n -> g p t n", p=P, t=PACK)
+    w_fc1_k = w_fc1_bytes.rearrange("(g p t) n -> g p t n", p=P, t=PACK)
+
+    with ExitStack() as ctx:
+        keep = ctx.enter_context(tc.tile_pool(name="keep", bufs=1))
+        work = ctx.enter_context(tc.tile_pool(name="work", bufs=2))
+        psum = ctx.enter_context(tc.psum_pool(name="psum", bufs=8))
+        ctx.enter_context(tc.manual_schedule(engines={mybir.EngineType.SP}))
+
+        planes, grouped, codes, scales = {}, {}, {}, {}
+        attn_sb, x_sb, w_bytes, attn_grouped, attn_codes, attn_scales = {}, {}, {}, {}, {}, {}
+        resid, acc, x_mid, sums, neg_mean, sq_sum, std, rstd, normed, act = {}, {}, {}, {}, {}, {}, {}, {}, {}, {}
+
+        def rows(i):
+            return slice(i * P, (i + 1) * P)
+
+        def cols(j):
+            return slice(j * N, (j + 1) * N)
+
+        def new_bank():
+            return psum.tile([P, N], F32, name="bank")
+
+        def new_planes(key):
+            planes[key] = work.tile([P, PLANES * N], BF16, name="planes", bufs=4, align_bytes=64)
+
+        def load_w_proj(h, g):
+            if g == 0:
+                new_planes(("proj", h))
+            nc.sync.dma_start(
+                out=planes["proj", h][:].rearrange("p (g t n) -> p g t n", g=PASSES, t=PACK)[:, g],
+                in_=w_proj_k[g][:, :, cols(h)],
+            )
+
+        def load_attn(i):
+            attn_sb[i] = work.tile([P, D], BF16, name="attn_sb", bufs=5)
+            nc.sync.dma_start(out=attn_sb[i][:], in_=attn_rows[rows(i), :])
+
+        def load_x(i):
+            x_sb[i] = work.tile([P, D], BF16, name="x_sb", bufs=5)
+            nc.sync.dma_start(out=x_sb[i][:], in_=x_rows[rows(i), :])
+
+        def load_w_fc1(b, g):
+            w_bytes[b, g] = work.tile([P, PACK * BLOCK], U8, name="w_bytes", bufs=6)
+            nc.sync.dma_start(
+                out=w_bytes[b, g][:].rearrange("p (t n) -> p t n", t=PACK),
+                in_=w_fc1_k[g][:, :, b * BLOCK : (b + 1) * BLOCK],
+            )
+
+        def load_columns(name, vector, dtype):
+            tile = keep.tile([P, PASSES * PACK], dtype, name=name)
+            nc.sync.dma_start(
+                out=tile[:].rearrange("p (g t) -> p g t", t=PACK),
+                in_=vector.rearrange("(g p t) -> p g t", p=P, t=PACK),
+            )
+            return tile
+
+        def load_spread(name, vector, width):
+            tile = keep.tile([P, width], BF16, name=name)
+            nc.sync.dma_start(out=tile[:], in_=vector.partition_broadcast(P))
+            return tile
+
+        def new_grouped(key):
+            grouped[key] = work.tile([P, PLANES * N], BF16, name="grouped", bufs=2, align_bytes=64)
+
+        def in_runs(key, first, stop):
+            out = grouped[key][:].rearrange("p (c i t) -> p c t i", i=4, t=PACK)[:, first // 4 : stop // 4]
+            source = planes[key][:].rearrange("p (t c i) -> p c t i", i=4, t=PACK)[:, first // 4 : stop // 4]
+            return out, source
+
+        def interleave(key, passes):
+            nc.vector.tensor_copy(
+                out=grouped[key][:].rearrange("p (g c i t) -> p g c t i", g=PASSES, i=4, t=PACK)[:, passes],
+                in_=planes[key][:].rearrange("p (g t c i) -> p g c t i", g=PASSES, i=4, t=PACK)[:, passes],
+            )
+
+        def interleave_rest(key):
+            out, source = in_runs(key, POOL_COLS, PASSES * N)
+            nc.vector.tensor_copy(out=out, in_=source)
+
+        def interleave_on_scalar(key):
+            out, source = in_runs(key, POOL_COLS, PASSES * N)
+            nc.scalar.copy(out=out, in_=source)
+
+        def interleave_on_gpsimd(key):
+            nc.gpsimd.tensor_scalar(
+                out=grouped[key][:].rearrange("p (q t) -> p q t", t=PACK)[:, :POOL_COLS],
+                in0=planes[key][:].rearrange("p (t q) -> p q t", t=PACK)[:, :POOL_COLS],
+                scalar1=1.0,
+                scalar2=0.0,
+                op0=ALU.mult,
+                op1=ALU.add,
+            )
+
+        def quantize(key, passes):
+            kind = key[0]
+            if passes.start == 0:
+                codes[key] = work.tile([P, PASSES * N], U32, name=kind + "_codes", bufs=3 if kind == "fc1" else 2, align_bytes=64)
+                scales[key] = work.tile([P, PASSES * N], U8, name=kind + "_scales", bufs=3 if kind == "fc1" else 2, align_bytes=64)
+            words = slice(passes.start * N, passes.stop * N)
+            nc.vector.quantize_mx(
+                out=codes[key][:, words].bitcast(FP8X4),
+                scales=scales[key][:, words],
+                in_=grouped[key][:, PACK * words.start : PACK * words.stop],
+            )
+
+        def widen(c, plane, on_vector=False):
+            g, t = divmod(plane, PACK)
+            if ("fc1", c) not in planes:
+                new_planes(("fc1", c))
+            b, first = divmod(c * N, BLOCK)
+            source = w_bytes[b, g][:, t * BLOCK + first : t * BLOCK + first + N].bitcast(FP8)
+            scale = w_scale[:, plane : plane + 1]
+            target = planes["fc1", c][:, cols(plane if c < 2 else t * PASSES + g)]
+            if on_vector:
+                nc.vector.tensor_scalar(
+                    out=target, in0=source, scalar1=scale, scalar2=None, op0=ALU.mult
+                )
+            else:
+                nc.scalar.activation(out=target, in_=source, func=ACT.Copy, scale=scale)
+
+        def turn_attn(i):
+            words = attn_sb[i][:].bitcast(F32)
+            bank = new_bank()
+            for g in range(PASSES):
+                for u in range(2):
+                    j = 2 * g + u
+                    nc.tensor.transpose(
+                        bank[:, j * P : (j + 1) * P], words[:, 2 * P * g + u : 2 * P * (g + 1) : 2], ident_f32[:]
+                    )
+            attn_grouped[i] = work.tile([P, D], BF16, name="attn_grouped", bufs=3, align_bytes=64)
+            nc.scalar.copy(
+                out=attn_grouped[i][:].bitcast(F32).rearrange("p (g r u) -> p g r u", g=PASSES, u=2),
+                in_=bank[:].rearrange("p (g u r) -> p g r u", g=PASSES, u=2),
+            )
+
+        def quantize_attn(i):
+            attn_codes[i] = work.tile([P, PASSES * P], U32, name="attn_codes", bufs=3, align_bytes=64)
+            attn_scales[i] = work.tile([P, PASSES * P], U8, name="attn_scales", bufs=3, align_bytes=64)
+            nc.vector.quantize_mx(
+                out=attn_codes[i][:].bitcast(FP8X4), scales=attn_scales[i][:], in_=attn_grouped[i][:]
+            )
+
+        def residual(i):
+            for h in range(2):
+                bank = new_bank()
+                nc.tensor.matmul(bank[:], lhsT=ident_bf16[:], rhs=x_sb[i][:, cols(h)], start=True, stop=False)
+                nc.tensor.matmul(bank[:], lhsT=ident_bf16[:], rhs=b_proj_sb[:, cols(h)], start=False, stop=True)
+                resid[i, h] = work.tile([P, N], F32, name="staged", bufs=12)
+                nc.scalar.copy(out=resid[i, h][:], in_=bank[:])
+
+        def project(i, h):
+            acc["proj", i, h] = new_bank()
+            for g in range(PASSES):
+                nc.tensor.matmul_mx(
+                    out=acc["proj", i, h][:],
+                    lhsT=attn_codes[i][:, g * P : (g + 1) * P].bitcast(FP8X4),
+                    lhsT_scale=attn_scales[i][:, g * P : (g + 1) * P],
+                    rhs=codes["proj", h][:, cols(g)].bitcast(FP8X4),
+                    rhs_scale=scales["proj", h][:, cols(g)],
+                    start=(g == 0),
+                    stop=(g == PASSES - 1),
+                )
+
+        def add_residual(i, h):
+            if h == 0:
+                x_mid[i] = work.tile([P, D], F32, name="x_mid", bufs=6)
+                sums[i] = work.tile([P, 2], F32, name="sums")
+            nc.vector.scalar_tensor_tensor(
+                out=x_mid[i][:, cols(h)],
+                in0=acc["proj", i, h][:],
+                scalar=1.0,
+                in1=resid[i, h][:],
+                op0=ALU.mult,
+                op1=ALU.add,
+                accum_out=sums[i][:, h : h + 1],
+            )
+
+        def store_x_mid(i):
+            nc.sync.dma_start(out=x_mid_rows[rows(i), :], in_=x_mid[i][:])
+
+        def mean(i):
+            neg_mean[i] = work.tile([P, 1], F32, name="neg_mean", bufs=3)
+            nc.vector.tensor_scalar(
+                out=neg_mean[i][:],
+                in0=sums[i][:, 0:1],
+                scalar1=sums[i][:, 1:2],
+                scalar2=-1.0 / D,
+                op0=ALU.add,
+                op1=ALU.mult,
+            )
+
+        def square_sum(i):
+            sq_sum[i] = work.tile([P, 1], F32, name="sq_sum")
+            squares = work.tile([P, D], BF16, name="squares", bufs=1)
+            nc.scalar.activation(
+                out=squares[:], in_=x_mid[i][:], func=ACT.Square, bias=neg_mean[i][:], accum_out=sq_sum[i][:]
+            )
+
+        def deviation(i):
+            std[i] = work.tile([P, 1], F32, name="std")
+            nc.scalar.activation(out=std[i][:], in_=sq_sum[i][:], func=ACT.Sqrt, scale=1.0 / D, bias=EPS)
+
+        def invert(i):
+            rstd[i] = work.tile([P, 1], F32, name="rstd")
+            nc.vector.reciprocal(out=rstd[i][:], in_=std[i][:])
+
+        def normalise(i):
+            normed[i] = work.tile([P, D], F32, name="normed", bufs=6)
+            nc.vector.tensor_scalar(
+                out=normed[i][:].rearrange("r (t q) -> r q t", t=PACK),
+                in0=x_mid[i][:].rearrange("r (q t) -> r q t", t=PACK),
+                scalar1=neg_mean[i][:],
+                scalar2=rstd[i][:],
+                op0=ALU.add,
+                op1=ALU.mult,
+            )
+
+        def turn_normed(s, g, tiles=range(GROUP)):
+            for j in tiles:
+                for t in range(PACK):
+                    if j == 0:
+                        acc["h", s, g, t] = new_bank()
+                    first = (t * PASSES + g) * P
+                    nc.tensor.transpose(
+                        acc["h", s, g, t][:, j * P : (j + 1) * P],
+                        normed[s * GROUP + j][:, first : first + P],
+                        ident_f32[:],
+                    )
+
+        def gain_shift(s, g, t, on_vector=False):
+            if ("h", s) not in planes:
+                new_planes(("h", s))
+            plane = g * PACK + t
+            if on_vector:
+                nc.vector.tensor_scalar(
+                    out=planes["h", s][:, cols(plane)],
+                    in0=acc["h", s, g, t][:],
+                    scalar1=gain[:, plane : plane + 1],
+                    scalar2=shift[:, plane : plane + 1],
+                    op0=ALU.mult,
+                    op1=ALU.add,
+                )
+            else:
+                nc.scalar.activation(
+                    out=planes["h", s][:, cols(plane)],
+                    in_=acc["h", s, g, t][:],
+                    func=ACT.Identity,
+                    scale=gain[:, plane : plane + 1],
+                    bias=shift[:, plane : plane + 1],
+                )
+
+        def fc1(c, i):
+            s, j = divmod(i, GROUP)
+            acc["fc1", c, i] = new_bank()
+            for g in range(PASSES):
+                nc.tensor.matmul_mx(
+                    out=acc["fc1", c, i][:],
+                    lhsT=codes["h", s][:, g * N + j * P : g * N + (j + 1) * P].bitcast(FP8X4),
+                    lhsT_scale=scales["h", s][:, g * N + j * P : g * N + (j + 1) * P],
+                    rhs=codes["fc1", c][:, cols(g)].bitcast(FP8X4),
+                    rhs_scale=scales["fc1", c][:, cols(g)],
+                    start=(g == 0),
+                    stop=(g == PASSES - 1),
+                )
+
+        def add_bias(c, i):
+            act[c, i] = work.tile([P, N], F32, name="staged", bufs=12)
+            half, first = divmod(c * N, F // 2)
+            nc.vector.tensor_tensor(
+                out=act[c, i][:], in0=acc["fc1", c, i][:], in1=b_fc1_sb[half][:, first : first + N], op=ALU.add
+            )
+
+        def gelu(c, i):
+            nc.scalar.activation(out=act[c, i][:], in_=act[c, i][:], func=ACT.Gelu)
+            nc.sync.dma_start(out=hid_rows[rows(i), cols(c)], in_=act[c, i][:])
+
+        first_pass, second_pass, both = slice(0, 1), slice(1, 2), slice(0, 2)
+        load_w_proj(0, 0)
+        w_scale = load_columns("w_scale", w_fc1_scale.rearrange("k o -> (k o)"), F32)
+        load_w_fc1(0, 0)
+        load_w_proj(0, 1)
+        load_attn(0)
+        load_w_fc1(0, 1)
+        load_w_proj(1, 0)
+        b_proj_sb = load_spread("b_proj_sb", b_proj, D)
+        load_x(0)
+        load_w_proj(1, 1)
+        for i in range(1, 4):
+            load_attn(i)
+            load_x(i)
+        gain_bf16 = load_columns("gain_bf16", g2, BF16)
+        shift_bf16 = load_columns("shift_bf16", beta2, BF16)
+        load_attn(4)
+        load_x(4)
+        load_w_fc1(1, 0)
+        load_w_fc1(1, 1)
+
+        warm = keep.tile([P, 2], F32, name="warm")
+        nc.vector.memset(warm[:, 0:1], 1.0)
+        nc.scalar.activation(out=warm[:, 1:2], in_=warm[:, 0:1], func=ACT.Sqrt)
+        ident_f32 = keep.tile([P, P], F32, name="ident_f32")
+        make_identity(nc, ident_f32[:])
+        ident_bf16 = keep.tile([P, P], BF16, name="ident_bf16")
+        make_identity(nc, ident_bf16[:])
+
+        new_grouped(("proj", 0))
+        interleave(("proj", 0), first_pass)
+        for plane in range(PACK):
+            widen(0, plane)
+        turn_attn(0)
+        quantize(("proj", 0), first_pass)
+        interleave(("proj", 0), second_pass)
+        for plane in range(PACK):
+            widen(1, plane)
+        new_grouped(("fc1", 0))
+        interleave(("fc1", 0), first_pass)
+        quantize(("proj", 0), second_pass)
+        quantize_attn(0)
+        new_grouped(("proj", 1))
+        interleave(("proj", 1), first_pass)
+        quantize(("fc1", 0), first_pass)
+        residual(0)
+        project(0, 0)
+        quantize(("proj", 1), first_pass)
+        for plane in range(PACK, PLANES):
+            widen(0, plane)
+        turn_attn(1)
+        interleave(("proj", 1), second_pass)
+        add_residual(0, 0)
+        quantize(("proj", 1), second_pass)
+        quantize_attn(1)
+        turn_attn(2)
+
+        gain = keep.tile([P, PLANES], F32, name="gain")
+        shift = keep.tile([P, PLANES], F32, name="shift")
+        b_fc1_sb = {}
+        fc1_grouped = keep.tile([P, PLANES * N], BF16, name="fc1_grouped", align_bytes=64)
+        for c in range(1, CHUNKS):
+            grouped["fc1", c] = fc1_grouped
+        steps = [(c, i) for s in range(2) for c in range(2) for i in range(s * GROUP, (s + 1) * GROUP)]
+        steps.extend([(c, i) for c in range(2, CHUNKS) for i in range(TILES)])
+        last = TILES - 1
+        for i in range(TILES):
+            if i > 0:
+                project(i, 0)
+            project(i, 1)
+            if i + 1 < TILES:
+                residual(i + 1)
+            if i + 3 < TILES:
+                turn_attn(i + 3)
+            if i + 5 < TILES:
+                load_attn(i + 5)
+                load_x(i + 5)
+            if i == 3:
+                b_fc1_sb[0] = load_spread("b_fc1_low", b_fc1[: F // 2], F // 2)
+            if i > 0:
+                add_residual(i, 0)
+            add_residual(i, 1)
+            if i + 2 < TILES:
+                quantize_attn(i + 2)
+            mean(i)
+            if i > 0:
+                invert(i - 1)
+                normalise(i - 1)
+            if i >= 3:
+                store_x_mid(i - 3)
+            if i < last:
+                square_sum(i)
+                deviation(i)
+            if i == 0:
+                interleave(("fc1", 0), second_pass)
+                quantize(("fc1", 0), second_pass)
+                for plane in range(PACK, PLANES):
+                    widen(1, plane)
+            if i == 2:
+                nc.vector.tensor_copy(out=gain[:], in_=gain_bf16[:])
+                nc.vector.tensor_copy(out=shift[:], in_=shift_bf16[:])
+                interleave(("fc1", 1), first_pass)
+                interleave(("fc1", 1), second_pass)
+                quantize(("fc1", 1), both)
+            if i in (4, 5):
+                g = i - 4
+                turn_normed(0, g)
+                for t in range(PACK):
+                    gain_shift(0, g, t, on_vector=(t == PACK - 1))
+                if g == 0:
+                    new_grouped(("h", 0))
+                interleave(("h", 0), slice(g, g + 1))
+                quantize(("h", 0), slice(g, g + 1))
+            if i == 6:
+                for plane in range(VECTOR_PLANES, PLANES):
+                    widen(2, plane)
+        for i in range(TILES - 3, TILES):
+            store_x_mid(i)
+        b_fc1_sb[1] = load_spread("b_fc1_high", b_fc1[F // 2 :], F // 2)
+        load_w_fc1(2, 0)
+        load_w_fc1(2, 1)
+
+        ctx.enter_context(tc.manual_schedule())
+        square_sum(last)
+        fc1(*steps[0])
+        fc1(*steps[1])
+        turn_normed(1, 0, range(GROUP - 1))
+        widen(3, VECTOR_PLANES)
+        deviation(last)
+        widen(2, 0, on_vector=True)
+        widen(2, 1, on_vector=True)
+        add_bias(*steps[0])
+        gelu(*steps[0])
+        invert(last)
+        add_bias(*steps[1])
+        gelu(*steps[1])
+        normalise(last)
+        for plane in range(2, VECTOR_PLANES):
+            widen(2, plane, on_vector=True)
+        if POOL_COLS:
+            interleave_on_gpsimd(("fc1", 2))
+        fc1(*steps[2])
+        fc1(*steps[3])
+        turn_normed(1, 0, range(GROUP - 1, GROUP))
+        add_bias(*steps[2])
+        for t in range(PACK):
+            gain_shift(1, 0, t, on_vector=True)
+        add_bias(*steps[3])
+        turn_normed(1, 1)
+        gelu(*steps[2])
+        for t in range(PACK):
+            gain_shift(1, 1, t)
+        gelu(*steps[3])
+        for plane in range(VECTOR_PLANES + 1, PLANES):
+            widen(3, plane)
+        fc1(*steps[4])
+        fc1(*steps[5])
+        load_w_fc1(3, 0)
+        load_w_fc1(3, 1)
+
+        for n in range(GROUP, len(steps)):
+            window, place = divmod(n, TILES)
+            add_bias(*steps[n])
+            gelu(*steps[n])
+            due = window + 2
+            if place == TILES - 3 and due < CHUNKS:
+                if window == 0:
+                    new_grouped(("h", 1))
+                    interleave(("h", 1), both)
+                if due + 1 < CHUNKS:
+                    interleave_rest(("fc1", due))
+                if window == 0:
+                    quantize(("h", 1), both)
+                if due + 2 < CHUNKS:
+                    for plane in range(VECTOR_PLANES):
+                        widen(due + 1, plane, on_vector=True)
+                quantize(("fc1", due), both)
+                if due + 1 < CHUNKS and POOL_COLS:
+                    interleave_on_gpsimd(("fc1", due + 1))
+                if due + 2 < CHUNKS:
+                    for plane in range(VECTOR_PLANES if due + 3 < CHUNKS else 0, PLANES):
+                        widen(due + 2, plane)
+                if due + 2 == CHUNKS:
+                    interleave_on_scalar(("fc1", due + 1))
+            if n + 2 < len(steps):
+                fc1(*steps[n + 2])

@@ -22,11 +22,18 @@ PACK = 4
 PASSES = D // (P * PACK)
 N = 512
 TILES = T // P
-GROUP = N // P
 CHUNKS = F // N
+SPAN = 2
+HOUT_V = 2
+PAIRED = CHUNKS - 2
+OPT_A = 1
+OPT_B = 1
+FIRST = 2
+PLACE = 5
 BLOCK = 1024
 PLANES = PASSES * PACK
 POOL_COLS = 640
+CODE_BUFS = {"proj": 2, "h": 4, "fc1": 3}
 VECTOR_PLANES = 3
 
 
@@ -45,7 +52,7 @@ def tile_flashinferblock_pb_kernel(
         keep = ctx.enter_context(tc.tile_pool(name="keep", bufs=1))
         work = ctx.enter_context(tc.tile_pool(name="work", bufs=2))
         psum = ctx.enter_context(tc.psum_pool(name="psum", bufs=8))
-        ctx.enter_context(tc.manual_schedule(engines={mybir.EngineType.SP}))
+        ctx.enter_context(tc.manual_schedule(engines={mybir.EngineType.SP, mybir.EngineType.PE}))
 
         planes, grouped, codes, scales = {}, {}, {}, {}
         attn_sb, x_sb, w_bytes, attn_grouped, attn_codes, attn_scales = {}, {}, {}, {}, {}, {}
@@ -60,8 +67,12 @@ def tile_flashinferblock_pb_kernel(
         def new_bank():
             return psum.tile([P, N], F32, name="bank")
 
+        def width(key):
+            return SPAN * P if key[0] == "h" else N
+
         def new_planes(key):
-            planes[key] = work.tile([P, PLANES * N], BF16, name="planes", bufs=4, align_bytes=64)
+            name, bufs = ("h_planes", 2) if key[0] == "h" else ("planes", 4)
+            planes[key] = work.tile([P, PLANES * width(key)], BF16, name=name, bufs=bufs, align_bytes=64)
 
         def load_w_proj(h, g):
             if g == 0:
@@ -72,11 +83,11 @@ def tile_flashinferblock_pb_kernel(
             )
 
         def load_attn(i):
-            attn_sb[i] = work.tile([P, D], BF16, name="attn_sb", bufs=5)
+            attn_sb[i] = work.tile([P, D], BF16, name="attn_sb", tag="rows", bufs=22)
             nc.sync.dma_start(out=attn_sb[i][:], in_=attn_rows[rows(i), :])
 
         def load_x(i):
-            x_sb[i] = work.tile([P, D], BF16, name="x_sb", bufs=5)
+            x_sb[i] = work.tile([P, D], BF16, name="x_sb", tag="rows", bufs=22)
             nc.sync.dma_start(out=x_sb[i][:], in_=x_rows[rows(i), :])
 
         def load_w_fc1(b, g):
@@ -88,7 +99,7 @@ def tile_flashinferblock_pb_kernel(
 
         def load_columns(name, vector, dtype):
             tile = keep.tile([P, PASSES * PACK], dtype, name=name)
-            nc.sync.dma_start(
+            nc.scalar.dma_start(
                 out=tile[:].rearrange("p (g t) -> p g t", t=PACK),
                 in_=vector.rearrange("(g p t) -> p g t", p=P, t=PACK),
             )
@@ -100,7 +111,7 @@ def tile_flashinferblock_pb_kernel(
             return tile
 
         def new_grouped(key):
-            grouped[key] = work.tile([P, PLANES * N], BF16, name="grouped", bufs=2, align_bytes=64)
+            grouped[key] = work.tile([P, PLANES * width(key)], BF16, name="grouped", bufs=2, align_bytes=64)
 
         def in_runs(key, first, stop):
             out = grouped[key][:].rearrange("p (c i t) -> p c t i", i=4, t=PACK)[:, first // 4 : stop // 4]
@@ -134,9 +145,9 @@ def tile_flashinferblock_pb_kernel(
         def quantize(key, passes):
             kind = key[0]
             if passes.start == 0:
-                codes[key] = work.tile([P, PASSES * N], U32, name=kind + "_codes", bufs=3 if kind == "fc1" else 2, align_bytes=64)
-                scales[key] = work.tile([P, PASSES * N], U8, name=kind + "_scales", bufs=3 if kind == "fc1" else 2, align_bytes=64)
-            words = slice(passes.start * N, passes.stop * N)
+                codes[key] = work.tile([P, PASSES * width(key)], U32, name=kind + "_codes", bufs=CODE_BUFS[kind], align_bytes=64)
+                scales[key] = work.tile([P, PASSES * width(key)], U8, name=kind + "_scales", bufs=CODE_BUFS[kind], align_bytes=64)
+            words = slice(passes.start * width(key), passes.stop * width(key))
             nc.vector.quantize_mx(
                 out=codes[key][:, words].bitcast(FP8X4),
                 scales=scales[key][:, words],
@@ -150,7 +161,7 @@ def tile_flashinferblock_pb_kernel(
             b, first = divmod(c * N, BLOCK)
             source = w_bytes[b, g][:, t * BLOCK + first : t * BLOCK + first + N].bitcast(FP8)
             scale = w_scale[:, plane : plane + 1]
-            target = planes["fc1", c][:, cols(plane if c < 2 else t * PASSES + g)]
+            target = planes["fc1", c][:, cols(plane if c < FIRST else t * PASSES + g)]
             if on_vector:
                 nc.vector.tensor_scalar(
                     out=target, in0=source, scalar1=scale, scalar2=None, op0=ALU.mult
@@ -184,8 +195,8 @@ def tile_flashinferblock_pb_kernel(
             for h in range(2):
                 bank = new_bank()
                 nc.tensor.matmul(bank[:], lhsT=ident_bf16[:], rhs=x_sb[i][:, cols(h)], start=True, stop=False)
-                nc.tensor.matmul(bank[:], lhsT=ident_bf16[:], rhs=b_proj_sb[:, cols(h)], start=False, stop=True)
-                resid[i, h] = work.tile([P, N], F32, name="staged", bufs=12)
+                nc.tensor.matmul(bank[:], lhsT=ones[:], rhs=b_proj_row[:, cols(h)], start=False, stop=True)
+                resid[i, h] = work.tile([P, N], F32, name="staged", tag="rows", bufs=22)
                 nc.scalar.copy(out=resid[i, h][:], in_=bank[:])
 
         def project(i, h):
@@ -245,7 +256,7 @@ def tile_flashinferblock_pb_kernel(
             nc.vector.reciprocal(out=rstd[i][:], in_=std[i][:])
 
         def normalise(i):
-            normed[i] = work.tile([P, D], F32, name="normed", bufs=6)
+            normed[i] = work.tile([P, D], F32, name="normed", bufs=4)
             nc.vector.tensor_scalar(
                 out=normed[i][:].rearrange("r (t q) -> r q t", t=PACK),
                 in0=x_mid[i][:].rearrange("r (q t) -> r q t", t=PACK),
@@ -255,26 +266,29 @@ def tile_flashinferblock_pb_kernel(
                 op1=ALU.mult,
             )
 
-        def turn_normed(s, g, tiles=range(GROUP)):
+        def turn_normed(s, tiles=range(SPAN)):
             for j in tiles:
-                for t in range(PACK):
-                    if j == 0:
-                        acc["h", s, g, t] = new_bank()
+                for plane in range(PLANES):
+                    g, t = divmod(plane, PACK)
+                    if j == 0 and plane % 2 == 0:
+                        acc["h", s, plane // 2] = new_bank()
                     first = (t * PASSES + g) * P
+                    column = (plane % 2 * SPAN + j) * P
                     nc.tensor.transpose(
-                        acc["h", s, g, t][:, j * P : (j + 1) * P],
-                        normed[s * GROUP + j][:, first : first + P],
+                        acc["h", s, plane // 2][:, column : column + P],
+                        normed[s * SPAN + j][:, first : first + P],
                         ident_f32[:],
                     )
 
-        def gain_shift(s, g, t, on_vector=False):
+        def gain_shift(s, plane, on_vector=False):
             if ("h", s) not in planes:
                 new_planes(("h", s))
-            plane = g * PACK + t
+            source = acc["h", s, plane // 2][:, plane % 2 * SPAN * P : (plane % 2 + 1) * SPAN * P]
+            target = planes["h", s][:, plane * SPAN * P : (plane + 1) * SPAN * P]
             if on_vector:
                 nc.vector.tensor_scalar(
-                    out=planes["h", s][:, cols(plane)],
-                    in0=acc["h", s, g, t][:],
+                    out=target,
+                    in0=source,
                     scalar1=gain[:, plane : plane + 1],
                     scalar2=shift[:, plane : plane + 1],
                     op0=ALU.mult,
@@ -282,21 +296,21 @@ def tile_flashinferblock_pb_kernel(
                 )
             else:
                 nc.scalar.activation(
-                    out=planes["h", s][:, cols(plane)],
-                    in_=acc["h", s, g, t][:],
+                    out=target,
+                    in_=source,
                     func=ACT.Identity,
                     scale=gain[:, plane : plane + 1],
                     bias=shift[:, plane : plane + 1],
                 )
 
         def fc1(c, i):
-            s, j = divmod(i, GROUP)
+            s, j = divmod(i, SPAN)
             acc["fc1", c, i] = new_bank()
             for g in range(PASSES):
                 nc.tensor.matmul_mx(
                     out=acc["fc1", c, i][:],
-                    lhsT=codes["h", s][:, g * N + j * P : g * N + (j + 1) * P].bitcast(FP8X4),
-                    lhsT_scale=scales["h", s][:, g * N + j * P : g * N + (j + 1) * P],
+                    lhsT=codes["h", s][:, (g * SPAN + j) * P : (g * SPAN + j + 1) * P].bitcast(FP8X4),
+                    lhsT_scale=scales["h", s][:, (g * SPAN + j) * P : (g * SPAN + j + 1) * P],
                     rhs=codes["fc1", c][:, cols(g)].bitcast(FP8X4),
                     rhs_scale=scales["fc1", c][:, cols(g)],
                     start=(g == 0),
@@ -304,32 +318,60 @@ def tile_flashinferblock_pb_kernel(
                 )
 
         def add_bias(c, i):
-            act[c, i] = work.tile([P, N], F32, name="staged", bufs=12)
+            if c < PAIRED:
+                tile = work.tile([P, N], F32, name="staged", tag="rows", bufs=22)
+                act[c, i] = tile[:]
+            elif c == PAIRED:
+                tile = work.tile([P, D], F32, name="staged_pair", tag="x_mid", bufs=6)
+                act["pair", i], act[c, i], act[c + 1, i] = tile[:], tile[:, :N], tile[:, N:]
             half, first = divmod(c * N, F // 2)
             nc.vector.tensor_tensor(
-                out=act[c, i][:], in0=acc["fc1", c, i][:], in1=b_fc1_sb[half][:, first : first + N], op=ALU.add
+                out=act[c, i], in0=acc["fc1", c, i][:], in1=b_fc1_sb[half][:, first : first + N], op=ALU.add
             )
 
         def gelu(c, i):
-            nc.scalar.activation(out=act[c, i][:], in_=act[c, i][:], func=ACT.Gelu)
-            nc.sync.dma_start(out=hid_rows[rows(i), cols(c)], in_=act[c, i][:])
+            if c < PAIRED or i == TILES - 1:
+                nc.scalar.activation(out=act[c, i], in_=act[c, i], func=ACT.Gelu)
+                nc.sync.dma_start(out=hid_rows[rows(i), cols(c)], in_=act[c, i])
+            elif c > PAIRED:
+                nc.scalar.activation(out=act["pair", i], in_=act["pair", i], func=ACT.Gelu)
+                nc.sync.dma_start(out=hid_rows[rows(i), PAIRED * N :], in_=act["pair", i])
+
+        def prepare(due):
+            if due + 1 < CHUNKS or not OPT_A:
+                interleave_rest(("fc1", due))
+            if due + 2 < CHUNKS or (due + 1 < CHUNKS and not OPT_B):
+                for plane in range(VECTOR_PLANES):
+                    widen(due + 1, plane, on_vector=True)
+            quantize(("fc1", due), both)
+            if due + 1 < CHUNKS and POOL_COLS:
+                interleave_on_gpsimd(("fc1", due + 1))
+            if due + 2 < CHUNKS:
+                for plane in range(VECTOR_PLANES if due + 3 < CHUNKS or not OPT_B else 0, PLANES):
+                    widen(due + 2, plane)
+            if due + 2 == CHUNKS and OPT_A:
+                interleave_on_scalar(("fc1", due + 1))
 
         first_pass, second_pass, both = slice(0, 1), slice(1, 2), slice(0, 2)
-        load_w_proj(0, 0)
+        b_proj_row = keep.tile([P, D], BF16, name="b_proj_row")
+        nc.vector.memset(b_proj_row[:], 0.0)
+        ones = keep.tile([P, P], BF16, name="ones")
+        nc.vector.memset(ones[:], 1.0)
         w_scale = load_columns("w_scale", w_fc1_scale.rearrange("k o -> (k o)"), F32)
+        gain_bf16 = load_columns("gain_bf16", g2, BF16)
+        shift_bf16 = load_columns("shift_bf16", beta2, BF16)
+        nc.scalar.dma_start(out=b_proj_row[0:1, :], in_=b_proj.rearrange("(o d) -> o d", o=1))
+        load_w_proj(0, 0)
         load_w_fc1(0, 0)
         load_w_proj(0, 1)
         load_attn(0)
         load_w_fc1(0, 1)
         load_w_proj(1, 0)
-        b_proj_sb = load_spread("b_proj_sb", b_proj, D)
         load_x(0)
         load_w_proj(1, 1)
         for i in range(1, 4):
             load_attn(i)
             load_x(i)
-        gain_bf16 = load_columns("gain_bf16", g2, BF16)
-        shift_bf16 = load_columns("shift_bf16", beta2, BF16)
         load_attn(4)
         load_x(4)
         load_w_fc1(1, 0)
@@ -350,7 +392,7 @@ def tile_flashinferblock_pb_kernel(
         turn_attn(0)
         quantize(("proj", 0), first_pass)
         interleave(("proj", 0), second_pass)
-        for plane in range(PACK):
+        for plane in range(VECTOR_PLANES, PACK) if FIRST == 1 else range(PACK):
             widen(1, plane)
         new_grouped(("fc1", 0))
         interleave(("fc1", 0), first_pass)
@@ -377,8 +419,8 @@ def tile_flashinferblock_pb_kernel(
         fc1_grouped = keep.tile([P, PLANES * N], BF16, name="fc1_grouped", align_bytes=64)
         for c in range(1, CHUNKS):
             grouped["fc1", c] = fc1_grouped
-        steps = [(c, i) for s in range(2) for c in range(2) for i in range(s * GROUP, (s + 1) * GROUP)]
-        steps.extend([(c, i) for c in range(2, CHUNKS) for i in range(TILES)])
+        steps = [(c, i) for c in range(PAIRED) for i in range(TILES)]
+        steps.extend([(c, i) for i in range(TILES) for c in range(PAIRED, CHUNKS)])
         last = TILES - 1
         for i in range(TILES):
             if i > 0:
@@ -393,12 +435,20 @@ def tile_flashinferblock_pb_kernel(
                 load_x(i + 5)
             if i == 3:
                 b_fc1_sb[0] = load_spread("b_fc1_low", b_fc1[: F // 2], F // 2)
+            if i == 0:
+                nc.vector.tensor_copy(out=gain[:], in_=gain_bf16[:])
+                nc.vector.tensor_copy(out=shift[:], in_=shift_bf16[:])
             if i > 0:
                 add_residual(i, 0)
             add_residual(i, 1)
             if i + 2 < TILES:
                 quantize_attn(i + 2)
             mean(i)
+            if i >= 3 and i % SPAN == 1:
+                s = (i - 3) // SPAN
+                turn_normed(s)
+                for plane in range(PLANES):
+                    gain_shift(s, plane, on_vector=(plane >= PLANES - HOUT_V))
             if i > 0:
                 invert(i - 1)
                 normalise(i - 1)
@@ -412,22 +462,15 @@ def tile_flashinferblock_pb_kernel(
                 quantize(("fc1", 0), second_pass)
                 for plane in range(PACK, PLANES):
                     widen(1, plane)
-            if i == 2:
-                nc.vector.tensor_copy(out=gain[:], in_=gain_bf16[:])
-                nc.vector.tensor_copy(out=shift[:], in_=shift_bf16[:])
+            if i == 2 and FIRST == 2:
                 interleave(("fc1", 1), first_pass)
                 interleave(("fc1", 1), second_pass)
                 quantize(("fc1", 1), both)
-            if i in (4, 5):
-                g = i - 4
-                turn_normed(0, g)
-                for t in range(PACK):
-                    gain_shift(0, g, t, on_vector=(t == PACK - 1))
-                if g == 0:
-                    new_grouped(("h", 0))
-                interleave(("h", 0), slice(g, g + 1))
-                quantize(("h", 0), slice(g, g + 1))
-            if i == 6:
+            if i >= 3 and i % SPAN == 1:
+                new_grouped(("h", s))
+                interleave(("h", s), both)
+                quantize(("h", s), both)
+            if i == 6 and FIRST == 2:
                 for plane in range(VECTOR_PLANES, PLANES):
                     widen(2, plane)
         for i in range(TILES - 3, TILES):
@@ -437,66 +480,61 @@ def tile_flashinferblock_pb_kernel(
         load_w_fc1(2, 1)
 
         ctx.enter_context(tc.manual_schedule())
+        s = last // SPAN
         square_sum(last)
         fc1(*steps[0])
         fc1(*steps[1])
-        turn_normed(1, 0, range(GROUP - 1))
-        widen(3, VECTOR_PLANES)
+        turn_normed(s, range(SPAN - 1))
+        widen(FIRST + 1, VECTOR_PLANES)
         deviation(last)
-        widen(2, 0, on_vector=True)
-        widen(2, 1, on_vector=True)
         add_bias(*steps[0])
         gelu(*steps[0])
-        invert(last)
+        for plane in range(VECTOR_PLANES - 1):
+            widen(FIRST, plane, on_vector=True)
         add_bias(*steps[1])
-        gelu(*steps[1])
-        normalise(last)
-        for plane in range(2, VECTOR_PLANES):
-            widen(2, plane, on_vector=True)
-        if POOL_COLS:
-            interleave_on_gpsimd(("fc1", 2))
+        invert(last)
         fc1(*steps[2])
         fc1(*steps[3])
-        turn_normed(1, 0, range(GROUP - 1, GROUP))
         add_bias(*steps[2])
-        for t in range(PACK):
-            gain_shift(1, 0, t, on_vector=True)
-        add_bias(*steps[3])
-        turn_normed(1, 1)
-        gelu(*steps[2])
-        for t in range(PACK):
-            gain_shift(1, 1, t)
-        gelu(*steps[3])
-        for plane in range(VECTOR_PLANES + 1, PLANES):
-            widen(3, plane)
+        normalise(last)
+        widen(FIRST, VECTOR_PLANES - 1, on_vector=True)
+        if POOL_COLS:
+            interleave_on_gpsimd(("fc1", FIRST))
         fc1(*steps[4])
+        turn_normed(s, range(SPAN - 1, SPAN))
+        add_bias(*steps[3])
+        gelu(*steps[1])
         fc1(*steps[5])
+        add_bias(*steps[4])
+        for plane in range(PLANES):
+            gain_shift(s, plane, on_vector=(plane >= PLANES - 4))
+        add_bias(*steps[5])
+        for n in range(2, 6):
+            gelu(*steps[n])
+            widen(FIRST + 1, VECTOR_PLANES + n - 1)
+        for plane in range(VECTOR_PLANES + 5, PLANES):
+            widen(FIRST + 1, plane)
+        new_grouped(("h", s))
+        interleave(("h", s), both)
+        interleave_rest(("fc1", FIRST))
+        quantize(("h", s), both)
+        for plane in range(VECTOR_PLANES):
+            widen(FIRST + 1, plane, on_vector=True)
+        quantize(("fc1", FIRST), both)
+        if POOL_COLS:
+            interleave_on_gpsimd(("fc1", FIRST + 1))
+        for plane in range(VECTOR_PLANES, PLANES):
+            widen(FIRST + 2, plane)
+        fc1(*steps[6])
+        fc1(*steps[7])
         load_w_fc1(3, 0)
         load_w_fc1(3, 1)
 
-        for n in range(GROUP, len(steps)):
+        for n in range(6, len(steps)):
             window, place = divmod(n, TILES)
             add_bias(*steps[n])
             gelu(*steps[n])
-            due = window + 2
-            if place == TILES - 3 and due < CHUNKS:
-                if window == 0:
-                    new_grouped(("h", 1))
-                    interleave(("h", 1), both)
-                if due + 1 < CHUNKS:
-                    interleave_rest(("fc1", due))
-                if window == 0:
-                    quantize(("h", 1), both)
-                if due + 2 < CHUNKS:
-                    for plane in range(VECTOR_PLANES):
-                        widen(due + 1, plane, on_vector=True)
-                quantize(("fc1", due), both)
-                if due + 1 < CHUNKS and POOL_COLS:
-                    interleave_on_gpsimd(("fc1", due + 1))
-                if due + 2 < CHUNKS:
-                    for plane in range(VECTOR_PLANES if due + 3 < CHUNKS else 0, PLANES):
-                        widen(due + 2, plane)
-                if due + 2 == CHUNKS:
-                    interleave_on_scalar(("fc1", due + 1))
+            if place == PLACE and window > 0 and window + FIRST < CHUNKS:
+                prepare(window + FIRST)
             if n + 2 < len(steps):
                 fc1(*steps[n + 2])

@@ -26,15 +26,21 @@ CHUNKS = F // N
 SPAN = 2
 HOUT_V = 2
 PAIRED = CHUNKS - 2
-OPT_A = 1
-OPT_B = 1
+VECTOR_COLS = 0
+LOOK = 4
+LAG = 2
+HEAD_V = 2
+EARLY = 3
+LAST_V = 8
+THIRD_V = 3
+TRANS_V = 6
 FIRST = 2
 PLACE = 5
 BLOCK = 1024
 PLANES = PASSES * PACK
 POOL_COLS = 640
 CODE_BUFS = {"proj": 2, "h": 4, "fc1": 3}
-VECTOR_PLANES = 3
+VECTOR_PLANES = 5
 
 
 def tile_flashinferblock_pb_kernel(
@@ -83,18 +89,19 @@ def tile_flashinferblock_pb_kernel(
             )
 
         def load_attn(i):
-            attn_sb[i] = work.tile([P, D], BF16, name="attn_sb", tag="rows", bufs=22)
+            attn_sb[i] = work.tile([P, D], BF16, name="attn_sb", tag="rows", bufs=16)
             nc.sync.dma_start(out=attn_sb[i][:], in_=attn_rows[rows(i), :])
 
         def load_x(i):
-            x_sb[i] = work.tile([P, D], BF16, name="x_sb", tag="rows", bufs=22)
+            x_sb[i] = work.tile([P, D], BF16, name="x_sb", tag="rows", bufs=16)
             nc.sync.dma_start(out=x_sb[i][:], in_=x_rows[rows(i), :])
 
-        def load_w_fc1(b, g):
-            w_bytes[b, g] = work.tile([P, PACK * BLOCK], U8, name="w_bytes", bufs=6)
+        def load_w_fc1(b, g, slots=slice(0, PACK)):
+            if slots.start == 0:
+                w_bytes[b, g] = work.tile([P, PACK * BLOCK], U8, name="w_bytes", bufs=6)
             nc.sync.dma_start(
-                out=w_bytes[b, g][:].rearrange("p (t n) -> p t n", t=PACK),
-                in_=w_fc1_k[g][:, :, b * BLOCK : (b + 1) * BLOCK],
+                out=w_bytes[b, g][:].rearrange("p (t n) -> p t n", t=PACK)[:, slots],
+                in_=w_fc1_k[g][:, slots, b * BLOCK : (b + 1) * BLOCK],
             )
 
         def load_columns(name, vector, dtype):
@@ -125,7 +132,7 @@ def tile_flashinferblock_pb_kernel(
             )
 
         def interleave_rest(key):
-            out, source = in_runs(key, POOL_COLS, PASSES * N)
+            out, source = in_runs(key, PASSES * N - VECTOR_COLS, PASSES * N)
             nc.vector.tensor_copy(out=out, in_=source)
 
         def interleave_on_scalar(key):
@@ -196,7 +203,7 @@ def tile_flashinferblock_pb_kernel(
                 bank = new_bank()
                 nc.tensor.matmul(bank[:], lhsT=ident_bf16[:], rhs=x_sb[i][:, cols(h)], start=True, stop=False)
                 nc.tensor.matmul(bank[:], lhsT=ones[:], rhs=b_proj_row[:, cols(h)], start=False, stop=True)
-                resid[i, h] = work.tile([P, N], F32, name="staged", tag="rows", bufs=22)
+                resid[i, h] = work.tile([P, N], F32, name="staged", tag="rows", bufs=16)
                 nc.scalar.copy(out=resid[i, h][:], in_=bank[:])
 
         def project(i, h):
@@ -214,7 +221,7 @@ def tile_flashinferblock_pb_kernel(
 
         def add_residual(i, h):
             if h == 0:
-                x_mid[i] = work.tile([P, D], F32, name="x_mid", bufs=6)
+                x_mid[i] = work.tile([P, D], F32, name="x_mid", tag="wide", bufs=13)
                 sums[i] = work.tile([P, 2], F32, name="sums")
             nc.vector.scalar_tensor_tensor(
                 out=x_mid[i][:, cols(h)],
@@ -256,7 +263,7 @@ def tile_flashinferblock_pb_kernel(
             nc.vector.reciprocal(out=rstd[i][:], in_=std[i][:])
 
         def normalise(i):
-            normed[i] = work.tile([P, D], F32, name="normed", bufs=4)
+            normed[i] = work.tile([P, D], F32, name="normed", tag="wide", bufs=13)
             nc.vector.tensor_scalar(
                 out=normed[i][:].rearrange("r (t q) -> r q t", t=PACK),
                 in0=x_mid[i][:].rearrange("r (q t) -> r q t", t=PACK),
@@ -317,40 +324,77 @@ def tile_flashinferblock_pb_kernel(
                     stop=(g == PASSES - 1),
                 )
 
-        def add_bias(c, i):
-            if c < PAIRED:
-                tile = work.tile([P, N], F32, name="staged", tag="rows", bufs=22)
-                act[c, i] = tile[:]
-            elif c == PAIRED:
-                tile = work.tile([P, D], F32, name="staged_pair", tag="x_mid", bufs=6)
-                act["pair", i], act[c, i], act[c + 1, i] = tile[:], tile[:, :N], tile[:, N:]
+        def add_bias(n):
+            c, i = steps[n]
+            if n % 2 == 0:
+                act[n // 2] = work.tile([P, 2 * N], F32, name="staged_pair", tag="wide", bufs=13)
             half, first = divmod(c * N, F // 2)
             nc.vector.tensor_tensor(
-                out=act[c, i], in0=acc["fc1", c, i][:], in1=b_fc1_sb[half][:, first : first + N], op=ALU.add
+                out=act[n // 2][:, cols(n % 2)],
+                in0=acc["fc1", c, i][:],
+                in1=b_fc1_sb[half][:, first : first + N],
+                op=ALU.add,
             )
 
-        def gelu(c, i):
-            if c < PAIRED or i == TILES - 1:
-                nc.scalar.activation(out=act[c, i], in_=act[c, i], func=ACT.Gelu)
-                nc.sync.dma_start(out=hid_rows[rows(i), cols(c)], in_=act[c, i])
-            elif c > PAIRED:
-                nc.scalar.activation(out=act["pair", i], in_=act["pair", i], func=ACT.Gelu)
-                nc.sync.dma_start(out=hid_rows[rows(i), PAIRED * N :], in_=act["pair", i])
+        def gelu(n):
+            c, i = steps[n]
+            if n + 2 >= len(steps):
+                tile = act[n // 2][:, cols(n % 2)]
+                nc.scalar.activation(out=tile, in_=tile, func=ACT.Gelu)
+                nc.sync.dma_start(out=hid_rows[rows(i), cols(c)], in_=tile)
+            elif n % 2:
+                tile = act[n // 2][:]
+                nc.scalar.activation(out=tile, in_=tile, func=ACT.Gelu)
+                if c < PAIRED:
+                    nc.sync.dma_start(
+                        out=hid_rows[(i - 1) * P : (i + 1) * P, cols(c)].rearrange("(j p) f -> p j f", p=P),
+                        in_=tile.rearrange("p (j f) -> p j f", j=2),
+                    )
+                else:
+                    nc.sync.dma_start(out=hid_rows[rows(i), PAIRED * N :], in_=tile)
+
+        def interleave_on_tensor(key):
+            source = planes[key][:].rearrange("p (t q) -> p q t", t=PACK)
+            for first in range(POOL_COLS, PASSES * N - VECTOR_COLS, 2 * P):
+                stop = min(first + 2 * P, PASSES * N - VECTOR_COLS)
+                bank = psum.tile([P, PACK * (stop - first)], BF16, name="bank")
+                acc[key, first] = bank
+                for q in range(first, stop, P):
+                    nc.tensor.matmul(
+                        bank[:, PACK * (q - first) : PACK * (q - first + P)],
+                        lhsT=ident_bf16[:],
+                        rhs=source[:, q : q + P],
+                        start=True,
+                        stop=True,
+                    )
+
+        def collect(key):
+            for first in range(POOL_COLS, PASSES * N - VECTOR_COLS, 2 * P):
+                stop = min(first + 2 * P, PASSES * N - VECTOR_COLS)
+                nc.scalar.copy(out=grouped[key][:, PACK * first : PACK * stop], in_=acc[key, first][:])
+
+        def issue_matmuls(upto):
+            while issued[0] < min(upto, len(steps)):
+                c, i = steps[issued[0]]
+                if ("fc1", c) not in codes or ("h", i // SPAN) not in codes:
+                    return
+                fc1(c, i)
+                issued[0] = issued[0] + 1
 
         def prepare(due):
-            if due + 1 < CHUNKS or not OPT_A:
+            if VECTOR_COLS:
                 interleave_rest(("fc1", due))
-            if due + 2 < CHUNKS or (due + 1 < CHUNKS and not OPT_B):
+            if due + 1 < CHUNKS:
                 for plane in range(VECTOR_PLANES):
-                    widen(due + 1, plane, on_vector=True)
+                    widen(due + 1, plane, on_vector=(due + 2 < CHUNKS or plane < LAST_V))
             quantize(("fc1", due), both)
-            if due + 1 < CHUNKS and POOL_COLS:
+            if due + 1 < CHUNKS:
                 interleave_on_gpsimd(("fc1", due + 1))
             if due + 2 < CHUNKS:
-                for plane in range(VECTOR_PLANES if due + 3 < CHUNKS or not OPT_B else 0, PLANES):
+                for plane in range(VECTOR_PLANES, PLANES):
                     widen(due + 2, plane)
-            if due + 2 == CHUNKS and OPT_A:
-                interleave_on_scalar(("fc1", due + 1))
+            if due + 1 < CHUNKS:
+                interleave_on_tensor(("fc1", due + 1))
 
         first_pass, second_pass, both = slice(0, 1), slice(1, 2), slice(0, 2)
         b_proj_row = keep.tile([P, D], BF16, name="b_proj_row")
@@ -361,8 +405,9 @@ def tile_flashinferblock_pb_kernel(
         gain_bf16 = load_columns("gain_bf16", g2, BF16)
         shift_bf16 = load_columns("shift_bf16", beta2, BF16)
         nc.scalar.dma_start(out=b_proj_row[0:1, :], in_=b_proj.rearrange("(o d) -> o d", o=1))
+        load_w_fc1(0, 0, slice(0, 2))
         load_w_proj(0, 0)
-        load_w_fc1(0, 0)
+        load_w_fc1(0, 0, slice(2, PACK))
         load_w_proj(0, 1)
         load_attn(0)
         load_w_fc1(0, 1)
@@ -385,14 +430,20 @@ def tile_flashinferblock_pb_kernel(
         ident_bf16 = keep.tile([P, P], BF16, name="ident_bf16")
         make_identity(nc, ident_bf16[:])
 
+        widen(0, 0)
+        for plane in range(HEAD_V):
+            widen(1, plane, on_vector=True)
+        widen(0, 1)
+        for plane in range(HEAD_V, 2):
+            widen(1, plane)
         new_grouped(("proj", 0))
         interleave(("proj", 0), first_pass)
-        for plane in range(PACK):
+        for plane in range(2, PACK):
             widen(0, plane)
         turn_attn(0)
         quantize(("proj", 0), first_pass)
         interleave(("proj", 0), second_pass)
-        for plane in range(VECTOR_PLANES, PACK) if FIRST == 1 else range(PACK):
+        for plane in range(2, PACK):
             widen(1, plane)
         new_grouped(("fc1", 0))
         interleave(("fc1", 0), first_pass)
@@ -419,13 +470,18 @@ def tile_flashinferblock_pb_kernel(
         fc1_grouped = keep.tile([P, PLANES * N], BF16, name="fc1_grouped", align_bytes=64)
         for c in range(1, CHUNKS):
             grouped["fc1", c] = fc1_grouped
-        steps = [(c, i) for c in range(PAIRED) for i in range(TILES)]
+        steps = [(c, i) for c in range(2) for i in range(TILES - SPAN)]
+        steps.extend([(c, i) for c in range(2) for i in range(TILES - SPAN, TILES)])
+        steps.extend([(c, i) for c in range(2, PAIRED) for i in range(TILES)])
         steps.extend([(c, i) for i in range(TILES) for c in range(PAIRED, CHUNKS)])
+        issued = [0]
         last = TILES - 1
         for i in range(TILES):
             if i > 0:
                 project(i, 0)
             project(i, 1)
+            if i == last:
+                issue_matmuls(2)
             if i + 1 < TILES:
                 residual(i + 1)
             if i + 3 < TILES:
@@ -471,7 +527,7 @@ def tile_flashinferblock_pb_kernel(
                 interleave(("h", s), both)
                 quantize(("h", s), both)
             if i == 6 and FIRST == 2:
-                for plane in range(VECTOR_PLANES, PLANES):
+                for plane in range(EARLY, PLANES):
                     widen(2, plane)
         for i in range(TILES - 3, TILES):
             store_x_mid(i)
@@ -482,59 +538,59 @@ def tile_flashinferblock_pb_kernel(
         ctx.enter_context(tc.manual_schedule())
         s = last // SPAN
         square_sum(last)
-        fc1(*steps[0])
-        fc1(*steps[1])
+        add_bias(0)
+        add_bias(1)
         turn_normed(s, range(SPAN - 1))
-        widen(FIRST + 1, VECTOR_PLANES)
+        widen(3, THIRD_V)
         deviation(last)
-        add_bias(*steps[0])
-        gelu(*steps[0])
-        for plane in range(VECTOR_PLANES - 1):
-            widen(FIRST, plane, on_vector=True)
-        add_bias(*steps[1])
+        gelu(1)
+        for plane in range(EARLY - 1):
+            widen(2, plane, on_vector=True)
         invert(last)
-        fc1(*steps[2])
-        fc1(*steps[3])
-        add_bias(*steps[2])
+        issue_matmuls(4)
+        add_bias(2)
         normalise(last)
-        widen(FIRST, VECTOR_PLANES - 1, on_vector=True)
-        if POOL_COLS:
-            interleave_on_gpsimd(("fc1", FIRST))
-        fc1(*steps[4])
+        widen(2, EARLY - 1, on_vector=True)
+        interleave_on_gpsimd(("fc1", 2))
+        issue_matmuls(5)
         turn_normed(s, range(SPAN - 1, SPAN))
-        add_bias(*steps[3])
-        gelu(*steps[1])
-        fc1(*steps[5])
-        add_bias(*steps[4])
+        add_bias(3)
+        issue_matmuls(6)
+        add_bias(4)
         for plane in range(PLANES):
-            gain_shift(s, plane, on_vector=(plane >= PLANES - 4))
-        add_bias(*steps[5])
-        for n in range(2, 6):
-            gelu(*steps[n])
-            widen(FIRST + 1, VECTOR_PLANES + n - 1)
-        for plane in range(VECTOR_PLANES + 5, PLANES):
-            widen(FIRST + 1, plane)
+            gain_shift(s, plane, on_vector=(plane >= PLANES - TRANS_V))
+        add_bias(5)
+        interleave_on_tensor(("fc1", 2))
+        issue_matmuls(6 + LOOK)
+        gelu(3)
+        for plane in range(THIRD_V + 1, PLANES):
+            widen(3, plane)
+        gelu(5)
+        collect(("fc1", 2))
         new_grouped(("h", s))
         interleave(("h", s), both)
-        interleave_rest(("fc1", FIRST))
+        widen(3, 0, on_vector=True)
         quantize(("h", s), both)
-        for plane in range(VECTOR_PLANES):
-            widen(FIRST + 1, plane, on_vector=True)
-        quantize(("fc1", FIRST), both)
-        if POOL_COLS:
-            interleave_on_gpsimd(("fc1", FIRST + 1))
+        issue_matmuls(6 + LOOK)
+        if VECTOR_COLS:
+            interleave_rest(("fc1", 2))
+        for plane in range(1, THIRD_V):
+            widen(3, plane, on_vector=True)
+        quantize(("fc1", 2), both)
+        interleave_on_gpsimd(("fc1", 3))
         for plane in range(VECTOR_PLANES, PLANES):
-            widen(FIRST + 2, plane)
-        fc1(*steps[6])
-        fc1(*steps[7])
+            widen(4, plane)
+        interleave_on_tensor(("fc1", 3))
         load_w_fc1(3, 0)
         load_w_fc1(3, 1)
 
         for n in range(6, len(steps)):
             window, place = divmod(n, TILES)
-            add_bias(*steps[n])
-            gelu(*steps[n])
-            if place == PLACE and window > 0 and window + FIRST < CHUNKS:
-                prepare(window + FIRST)
-            if n + 2 < len(steps):
-                fc1(*steps[n + 2])
+            add_bias(n)
+            gelu(n)
+            if n >= PLACE + LAG and (n - PLACE - LAG) % TILES == 0 and (n - PLACE - LAG) // TILES + 3 < CHUNKS:
+                collect(("fc1", (n - PLACE - LAG) // TILES + 3))
+            issue_matmuls(n + 1 + LOOK)
+            if place == PLACE and window > 0 and window + 2 < CHUNKS:
+                prepare(window + 2)
+                issue_matmuls(n + 1 + LOOK)

@@ -20,27 +20,28 @@ ACT = mybir.ActivationFunctionType
 P = 128
 PACK = 4
 PASSES = D // (P * PACK)
+PLANES = PASSES * PACK
 N = 512
 TILES = T // P
 CHUNKS = F // N
+BLOCK = 2 * N
 SPAN = 2
-HOUT_V = 2
 PAIRED = CHUNKS - 2
-VECTOR_COLS = 0
-LOOK = 4
-LAG = 2
-HEAD_V = 2
-EARLY = 3
-LAST_V = 8
-THIRD_V = 3
-TRANS_V = 6
-FIRST = 2
-PLACE = 5
-BLOCK = 1024
-PLANES = PASSES * PACK
-POOL_COLS = 640
-CODE_BUFS = {"proj": 2, "h": 4, "fc1": 3}
-VECTOR_PLANES = 5
+SHARED = 2
+RUN = 4
+
+GPSIMD_COLS = 704
+TENSOR_COLS = 256
+VECTOR_PLANES = 2
+VECTOR_PLANES_FIRST = 3
+VECTOR_GAINS = 2
+VECTOR_GAINS_LAST = 6
+
+FIRST_RUN = TILES - SPAN
+LOOK = 6
+CODE_BUFS = {"proj": 2, "h": TILES // SPAN, "fc1": 3}
+ROW_BUFS = 16
+WIDE_BUFS = 13
 
 
 def tile_flashinferblock_pb_kernel(
@@ -62,7 +63,16 @@ def tile_flashinferblock_pb_kernel(
 
         planes, grouped, codes, scales = {}, {}, {}, {}
         attn_sb, x_sb, w_bytes, attn_grouped, attn_codes, attn_scales = {}, {}, {}, {}, {}, {}
-        resid, acc, x_mid, sums, neg_mean, sq_sum, std, rstd, normed, act = {}, {}, {}, {}, {}, {}, {}, {}, {}, {}
+        resid, acc, x_mid, sums, neg_mean, sq_sum, std, rstd, normed, staged = {}, {}, {}, {}, {}, {}, {}, {}, {}, {}
+        b_fc1_sb = {}
+        first_pass, second_pass, both = slice(0, 1), slice(1, 2), slice(0, 2)
+        last = TILES - 1
+
+        steps = [(c, i) for c in range(SHARED) for i in range(TILES - SPAN)]
+        steps.extend([(c, i) for c in range(SHARED) for i in range(TILES - SPAN, TILES)])
+        steps.extend([(c, i) for c in range(SHARED, PAIRED) for i in range(TILES)])
+        steps.extend([(c, i) for i in range(TILES) for c in range(PAIRED, CHUNKS)])
+        multiplied = []
 
         def rows(i):
             return slice(i * P, (i + 1) * P)
@@ -80,20 +90,23 @@ def tile_flashinferblock_pb_kernel(
             name, bufs = ("h_planes", 2) if key[0] == "h" else ("planes", 4)
             planes[key] = work.tile([P, PLANES * width(key)], BF16, name=name, bufs=bufs, align_bytes=64)
 
-        def load_w_proj(h, g):
+        def new_grouped(key):
+            grouped[key] = work.tile([P, PLANES * width(key)], BF16, name="grouped", bufs=2, align_bytes=64)
+
+        def load_w_proj(half, g):
             if g == 0:
-                new_planes(("proj", h))
+                new_planes(("proj", half))
             nc.sync.dma_start(
-                out=planes["proj", h][:].rearrange("p (g t n) -> p g t n", g=PASSES, t=PACK)[:, g],
-                in_=w_proj_k[g][:, :, cols(h)],
+                out=planes["proj", half][:].rearrange("p (g t n) -> p g t n", g=PASSES, t=PACK)[:, g],
+                in_=w_proj_k[g][:, :, cols(half)],
             )
 
         def load_attn(i):
-            attn_sb[i] = work.tile([P, D], BF16, name="attn_sb", tag="rows", bufs=16)
+            attn_sb[i] = work.tile([P, D], BF16, name="attn_sb", tag="rows", bufs=ROW_BUFS)
             nc.sync.dma_start(out=attn_sb[i][:], in_=attn_rows[rows(i), :])
 
         def load_x(i):
-            x_sb[i] = work.tile([P, D], BF16, name="x_sb", tag="rows", bufs=16)
+            x_sb[i] = work.tile([P, D], BF16, name="x_sb", tag="rows", bufs=ROW_BUFS)
             nc.sync.dma_start(out=x_sb[i][:], in_=x_rows[rows(i), :])
 
         def load_w_fc1(b, g, slots=slice(0, PACK)):
@@ -105,60 +118,17 @@ def tile_flashinferblock_pb_kernel(
             )
 
         def load_columns(name, vector, dtype):
-            tile = keep.tile([P, PASSES * PACK], dtype, name=name)
+            tile = keep.tile([P, PLANES], dtype, name=name)
             nc.scalar.dma_start(
                 out=tile[:].rearrange("p (g t) -> p g t", t=PACK),
                 in_=vector.rearrange("(g p t) -> p g t", p=P, t=PACK),
             )
             return tile
 
-        def load_spread(name, vector, width):
-            tile = keep.tile([P, width], BF16, name=name)
-            nc.sync.dma_start(out=tile[:], in_=vector.partition_broadcast(P))
-            return tile
-
-        def new_grouped(key):
-            grouped[key] = work.tile([P, PLANES * width(key)], BF16, name="grouped", bufs=2, align_bytes=64)
-
-        def in_runs(key, first, stop):
-            out = grouped[key][:].rearrange("p (c i t) -> p c t i", i=4, t=PACK)[:, first // 4 : stop // 4]
-            source = planes[key][:].rearrange("p (t c i) -> p c t i", i=4, t=PACK)[:, first // 4 : stop // 4]
-            return out, source
-
-        def interleave(key, passes):
-            nc.vector.tensor_copy(
-                out=grouped[key][:].rearrange("p (g c i t) -> p g c t i", g=PASSES, i=4, t=PACK)[:, passes],
-                in_=planes[key][:].rearrange("p (g t c i) -> p g c t i", g=PASSES, i=4, t=PACK)[:, passes],
-            )
-
-        def interleave_rest(key):
-            out, source = in_runs(key, PASSES * N - VECTOR_COLS, PASSES * N)
-            nc.vector.tensor_copy(out=out, in_=source)
-
-        def interleave_on_scalar(key):
-            out, source = in_runs(key, POOL_COLS, PASSES * N)
-            nc.scalar.copy(out=out, in_=source)
-
-        def interleave_on_gpsimd(key):
-            nc.gpsimd.tensor_scalar(
-                out=grouped[key][:].rearrange("p (q t) -> p q t", t=PACK)[:, :POOL_COLS],
-                in0=planes[key][:].rearrange("p (t q) -> p q t", t=PACK)[:, :POOL_COLS],
-                scalar1=1.0,
-                scalar2=0.0,
-                op0=ALU.mult,
-                op1=ALU.add,
-            )
-
-        def quantize(key, passes):
-            kind = key[0]
-            if passes.start == 0:
-                codes[key] = work.tile([P, PASSES * width(key)], U32, name=kind + "_codes", bufs=CODE_BUFS[kind], align_bytes=64)
-                scales[key] = work.tile([P, PASSES * width(key)], U8, name=kind + "_scales", bufs=CODE_BUFS[kind], align_bytes=64)
-            words = slice(passes.start * width(key), passes.stop * width(key))
-            nc.vector.quantize_mx(
-                out=codes[key][:, words].bitcast(FP8X4),
-                scales=scales[key][:, words],
-                in_=grouped[key][:, PACK * words.start : PACK * words.stop],
+        def load_b_fc1(half, name):
+            b_fc1_sb[half] = keep.tile([P, F // 2], BF16, name=name)
+            nc.sync.dma_start(
+                out=b_fc1_sb[half][:], in_=b_fc1[half * (F // 2) : (half + 1) * (F // 2)].partition_broadcast(P)
             )
 
         def widen(c, plane, on_vector=False):
@@ -168,13 +138,65 @@ def tile_flashinferblock_pb_kernel(
             b, first = divmod(c * N, BLOCK)
             source = w_bytes[b, g][:, t * BLOCK + first : t * BLOCK + first + N].bitcast(FP8)
             scale = w_scale[:, plane : plane + 1]
-            target = planes["fc1", c][:, cols(plane if c < FIRST else t * PASSES + g)]
+            target = planes["fc1", c][:, cols(plane if c < SHARED else t * PASSES + g)]
             if on_vector:
-                nc.vector.tensor_scalar(
-                    out=target, in0=source, scalar1=scale, scalar2=None, op0=ALU.mult
-                )
+                nc.vector.tensor_scalar(out=target, in0=source, scalar1=scale, scalar2=None, op0=ALU.mult)
             else:
                 nc.scalar.activation(out=target, in_=source, func=ACT.Copy, scale=scale)
+
+        def interleave(key, passes):
+            nc.vector.tensor_copy(
+                out=grouped[key][:].rearrange("p (g c i t) -> p g c t i", g=PASSES, i=RUN, t=PACK)[:, passes],
+                in_=planes[key][:].rearrange("p (g t c i) -> p g c t i", g=PASSES, i=RUN, t=PACK)[:, passes],
+            )
+
+        def interleave_on_gpsimd(c):
+            nc.gpsimd.tensor_scalar(
+                out=fc1_grouped[:].rearrange("p (q t) -> p q t", t=PACK)[:, :GPSIMD_COLS],
+                in0=planes["fc1", c][:].rearrange("p (t q) -> p q t", t=PACK)[:, :GPSIMD_COLS],
+                scalar1=1.0,
+                scalar2=0.0,
+                op0=ALU.mult,
+                op1=ALU.add,
+            )
+
+        def interleave_on_tensor(c):
+            source = planes["fc1", c][:].rearrange("p (t q) -> p q t", t=PACK)
+            acc["interleaved", c] = psum.tile([P, PACK * TENSOR_COLS], BF16, name="bank")
+            for q in range(0, TENSOR_COLS, P):
+                nc.tensor.matmul(
+                    acc["interleaved", c][:, PACK * q : PACK * (q + P)],
+                    lhsT=ident_bf16[:],
+                    rhs=source[:, GPSIMD_COLS + q : GPSIMD_COLS + q + P],
+                    start=True,
+                    stop=True,
+                )
+
+        def collect(c):
+            nc.vector.tensor_copy(
+                out=fc1_grouped[:, PACK * GPSIMD_COLS : PACK * (GPSIMD_COLS + TENSOR_COLS)],
+                in_=acc["interleaved", c][:],
+            )
+
+        def interleave_rest(c):
+            first = (GPSIMD_COLS + TENSOR_COLS) // RUN
+            nc.vector.tensor_copy(
+                out=fc1_grouped[:].rearrange("p (c i t) -> p c t i", i=RUN, t=PACK)[:, first:],
+                in_=planes["fc1", c][:].rearrange("p (t c i) -> p c t i", i=RUN, t=PACK)[:, first:],
+            )
+
+        def quantize(key, passes):
+            kind = key[0]
+            if passes.start == 0:
+                shape = [P, PASSES * width(key)]
+                codes[key] = work.tile(shape, U32, name=kind + "_codes", bufs=CODE_BUFS[kind], align_bytes=64)
+                scales[key] = work.tile(shape, U8, name=kind + "_scales", bufs=CODE_BUFS[kind], align_bytes=64)
+            words = slice(passes.start * width(key), passes.stop * width(key))
+            nc.vector.quantize_mx(
+                out=codes[key][:, words].bitcast(FP8X4),
+                scales=scales[key][:, words],
+                in_=grouped[key][:, PACK * words.start : PACK * words.stop],
+            )
 
         def turn_attn(i):
             words = attn_sb[i][:].bitcast(F32)
@@ -199,38 +221,38 @@ def tile_flashinferblock_pb_kernel(
             )
 
         def residual(i):
-            for h in range(2):
+            for half in range(2):
                 bank = new_bank()
-                nc.tensor.matmul(bank[:], lhsT=ident_bf16[:], rhs=x_sb[i][:, cols(h)], start=True, stop=False)
-                nc.tensor.matmul(bank[:], lhsT=ones[:], rhs=b_proj_row[:, cols(h)], start=False, stop=True)
-                resid[i, h] = work.tile([P, N], F32, name="staged", tag="rows", bufs=16)
-                nc.scalar.copy(out=resid[i, h][:], in_=bank[:])
+                nc.tensor.matmul(bank[:], lhsT=ident_bf16[:], rhs=x_sb[i][:, cols(half)], start=True, stop=False)
+                nc.tensor.matmul(bank[:], lhsT=ones[:], rhs=b_proj_row[:, cols(half)], start=False, stop=True)
+                resid[i, half] = work.tile([P, N], F32, name="staged", tag="rows", bufs=ROW_BUFS)
+                nc.scalar.copy(out=resid[i, half][:], in_=bank[:])
 
-        def project(i, h):
-            acc["proj", i, h] = new_bank()
+        def project(i, half):
+            acc["proj", i, half] = new_bank()
             for g in range(PASSES):
                 nc.tensor.matmul_mx(
-                    out=acc["proj", i, h][:],
+                    out=acc["proj", i, half][:],
                     lhsT=attn_codes[i][:, g * P : (g + 1) * P].bitcast(FP8X4),
                     lhsT_scale=attn_scales[i][:, g * P : (g + 1) * P],
-                    rhs=codes["proj", h][:, cols(g)].bitcast(FP8X4),
-                    rhs_scale=scales["proj", h][:, cols(g)],
+                    rhs=codes["proj", half][:, cols(g)].bitcast(FP8X4),
+                    rhs_scale=scales["proj", half][:, cols(g)],
                     start=(g == 0),
                     stop=(g == PASSES - 1),
                 )
 
-        def add_residual(i, h):
-            if h == 0:
-                x_mid[i] = work.tile([P, D], F32, name="x_mid", tag="wide", bufs=13)
+        def add_residual(i, half):
+            if half == 0:
+                x_mid[i] = work.tile([P, D], F32, name="x_mid", tag="wide", bufs=WIDE_BUFS)
                 sums[i] = work.tile([P, 2], F32, name="sums")
             nc.vector.scalar_tensor_tensor(
-                out=x_mid[i][:, cols(h)],
-                in0=acc["proj", i, h][:],
+                out=x_mid[i][:, cols(half)],
+                in0=acc["proj", i, half][:],
                 scalar=1.0,
-                in1=resid[i, h][:],
+                in1=resid[i, half][:],
                 op0=ALU.mult,
                 op1=ALU.add,
-                accum_out=sums[i][:, h : h + 1],
+                accum_out=sums[i][:, half : half + 1],
             )
 
         def store_x_mid(i):
@@ -263,7 +285,7 @@ def tile_flashinferblock_pb_kernel(
             nc.vector.reciprocal(out=rstd[i][:], in_=std[i][:])
 
         def normalise(i):
-            normed[i] = work.tile([P, D], F32, name="normed", tag="wide", bufs=13)
+            normed[i] = work.tile([P, D], F32, name="normed", tag="wide", bufs=WIDE_BUFS)
             nc.vector.tensor_scalar(
                 out=normed[i][:].rearrange("r (t q) -> r q t", t=PACK),
                 in0=x_mid[i][:].rearrange("r (q t) -> r q t", t=PACK),
@@ -287,63 +309,67 @@ def tile_flashinferblock_pb_kernel(
                         ident_f32[:],
                     )
 
-        def gain_shift(s, plane, on_vector=False):
-            if ("h", s) not in planes:
-                new_planes(("h", s))
-            source = acc["h", s, plane // 2][:, plane % 2 * SPAN * P : (plane % 2 + 1) * SPAN * P]
-            target = planes["h", s][:, plane * SPAN * P : (plane + 1) * SPAN * P]
-            if on_vector:
-                nc.vector.tensor_scalar(
-                    out=target,
-                    in0=source,
-                    scalar1=gain[:, plane : plane + 1],
-                    scalar2=shift[:, plane : plane + 1],
-                    op0=ALU.mult,
-                    op1=ALU.add,
-                )
-            else:
-                nc.scalar.activation(
-                    out=target,
-                    in_=source,
-                    func=ACT.Identity,
-                    scale=gain[:, plane : plane + 1],
-                    bias=shift[:, plane : plane + 1],
-                )
+        def gain_and_shift(s, on_vector):
+            new_planes(("h", s))
+            for plane in range(PLANES):
+                source = acc["h", s, plane // 2][:, plane % 2 * SPAN * P : (plane % 2 + 1) * SPAN * P]
+                target = planes["h", s][:, plane * SPAN * P : (plane + 1) * SPAN * P]
+                if plane >= PLANES - on_vector:
+                    nc.vector.tensor_scalar(
+                        out=target,
+                        in0=source,
+                        scalar1=gain[:, plane : plane + 1],
+                        scalar2=shift[:, plane : plane + 1],
+                        op0=ALU.mult,
+                        op1=ALU.add,
+                    )
+                else:
+                    nc.scalar.activation(
+                        out=target,
+                        in_=source,
+                        func=ACT.Identity,
+                        scale=gain[:, plane : plane + 1],
+                        bias=shift[:, plane : plane + 1],
+                    )
 
-        def fc1(c, i):
-            s, j = divmod(i, SPAN)
-            acc["fc1", c, i] = new_bank()
-            for g in range(PASSES):
-                nc.tensor.matmul_mx(
-                    out=acc["fc1", c, i][:],
-                    lhsT=codes["h", s][:, (g * SPAN + j) * P : (g * SPAN + j + 1) * P].bitcast(FP8X4),
-                    lhsT_scale=scales["h", s][:, (g * SPAN + j) * P : (g * SPAN + j + 1) * P],
-                    rhs=codes["fc1", c][:, cols(g)].bitcast(FP8X4),
-                    rhs_scale=scales["fc1", c][:, cols(g)],
-                    start=(g == 0),
-                    stop=(g == PASSES - 1),
-                )
+        def multiply_up_to(stop):
+            while len(multiplied) < min(stop, len(steps)):
+                c, i = steps[len(multiplied)]
+                s, j = divmod(i, SPAN)
+                if ("fc1", c) not in codes or ("h", s) not in codes:
+                    return
+                bank = new_bank()
+                for g in range(PASSES):
+                    nc.tensor.matmul_mx(
+                        out=bank[:],
+                        lhsT=codes["h", s][:, (g * SPAN + j) * P : (g * SPAN + j + 1) * P].bitcast(FP8X4),
+                        lhsT_scale=scales["h", s][:, (g * SPAN + j) * P : (g * SPAN + j + 1) * P],
+                        rhs=codes["fc1", c][:, cols(g)].bitcast(FP8X4),
+                        rhs_scale=scales["fc1", c][:, cols(g)],
+                        start=(g == 0),
+                        stop=(g == PASSES - 1),
+                    )
+                multiplied.append(bank)
 
         def add_bias(n):
-            c, i = steps[n]
             if n % 2 == 0:
-                act[n // 2] = work.tile([P, 2 * N], F32, name="staged_pair", tag="wide", bufs=13)
-            half, first = divmod(c * N, F // 2)
+                staged[n // 2] = work.tile([P, 2 * N], F32, name="staged_pair", tag="wide", bufs=WIDE_BUFS)
+            half, first = divmod(steps[n][0] * N, F // 2)
             nc.vector.tensor_tensor(
-                out=act[n // 2][:, cols(n % 2)],
-                in0=acc["fc1", c, i][:],
+                out=staged[n // 2][:, cols(n % 2)],
+                in0=multiplied[n][:],
                 in1=b_fc1_sb[half][:, first : first + N],
                 op=ALU.add,
             )
 
-        def gelu(n):
+        def gelu_and_store(n):
             c, i = steps[n]
             if n + 2 >= len(steps):
-                tile = act[n // 2][:, cols(n % 2)]
+                tile = staged[n // 2][:, cols(n % 2)]
                 nc.scalar.activation(out=tile, in_=tile, func=ACT.Gelu)
                 nc.sync.dma_start(out=hid_rows[rows(i), cols(c)], in_=tile)
             elif n % 2:
-                tile = act[n // 2][:]
+                tile = staged[n // 2][:]
                 nc.scalar.activation(out=tile, in_=tile, func=ACT.Gelu)
                 if c < PAIRED:
                     nc.sync.dma_start(
@@ -353,50 +379,20 @@ def tile_flashinferblock_pb_kernel(
                 else:
                     nc.sync.dma_start(out=hid_rows[rows(i), PAIRED * N :], in_=tile)
 
-        def interleave_on_tensor(key):
-            source = planes[key][:].rearrange("p (t q) -> p q t", t=PACK)
-            for first in range(POOL_COLS, PASSES * N - VECTOR_COLS, 2 * P):
-                stop = min(first + 2 * P, PASSES * N - VECTOR_COLS)
-                bank = psum.tile([P, PACK * (stop - first)], BF16, name="bank")
-                acc[key, first] = bank
-                for q in range(first, stop, P):
-                    nc.tensor.matmul(
-                        bank[:, PACK * (q - first) : PACK * (q - first + P)],
-                        lhsT=ident_bf16[:],
-                        rhs=source[:, q : q + P],
-                        start=True,
-                        stop=True,
-                    )
-
-        def collect(key):
-            for first in range(POOL_COLS, PASSES * N - VECTOR_COLS, 2 * P):
-                stop = min(first + 2 * P, PASSES * N - VECTOR_COLS)
-                nc.scalar.copy(out=grouped[key][:, PACK * first : PACK * stop], in_=acc[key, first][:])
-
-        def issue_matmuls(upto):
-            while issued[0] < min(upto, len(steps)):
-                c, i = steps[issued[0]]
-                if ("fc1", c) not in codes or ("h", i // SPAN) not in codes:
-                    return
-                fc1(c, i)
-                issued[0] = issued[0] + 1
-
-        def prepare(due):
-            if VECTOR_COLS:
-                interleave_rest(("fc1", due))
-            if due + 1 < CHUNKS:
+        def finish_chunk(c):
+            interleave_rest(c)
+            if c + 1 < CHUNKS:
                 for plane in range(VECTOR_PLANES):
-                    widen(due + 1, plane, on_vector=(due + 2 < CHUNKS or plane < LAST_V))
-            quantize(("fc1", due), both)
-            if due + 1 < CHUNKS:
-                interleave_on_gpsimd(("fc1", due + 1))
-            if due + 2 < CHUNKS:
+                    widen(c + 1, plane, on_vector=True)
+            quantize(("fc1", c), both)
+            if c + 1 < CHUNKS:
+                interleave_on_gpsimd(c + 1)
+            if c + 2 < CHUNKS:
                 for plane in range(VECTOR_PLANES, PLANES):
-                    widen(due + 2, plane)
-            if due + 1 < CHUNKS:
-                interleave_on_tensor(("fc1", due + 1))
+                    widen(c + 2, plane)
+            if c + 1 < CHUNKS:
+                interleave_on_tensor(c + 1)
 
-        first_pass, second_pass, both = slice(0, 1), slice(1, 2), slice(0, 2)
         b_proj_row = keep.tile([P, D], BF16, name="b_proj_row")
         nc.vector.memset(b_proj_row[:], 0.0)
         ones = keep.tile([P, P], BF16, name="ones")
@@ -414,28 +410,22 @@ def tile_flashinferblock_pb_kernel(
         load_w_proj(1, 0)
         load_x(0)
         load_w_proj(1, 1)
-        for i in range(1, 4):
+        for i in range(1, 5):
             load_attn(i)
             load_x(i)
-        load_attn(4)
-        load_x(4)
         load_w_fc1(1, 0)
         load_w_fc1(1, 1)
 
-        warm = keep.tile([P, 2], F32, name="warm")
-        nc.vector.memset(warm[:, 0:1], 1.0)
-        nc.scalar.activation(out=warm[:, 1:2], in_=warm[:, 0:1], func=ACT.Sqrt)
+        nc.scalar.activation(out=ones[:], in_=ones[:], func=ACT.Sqrt)
         ident_f32 = keep.tile([P, P], F32, name="ident_f32")
         make_identity(nc, ident_f32[:])
         ident_bf16 = keep.tile([P, P], BF16, name="ident_bf16")
         make_identity(nc, ident_bf16[:])
 
         widen(0, 0)
-        for plane in range(HEAD_V):
-            widen(1, plane, on_vector=True)
+        widen(1, 0, on_vector=True)
+        widen(1, 1, on_vector=True)
         widen(0, 1)
-        for plane in range(HEAD_V, 2):
-            widen(1, plane)
         new_grouped(("proj", 0))
         interleave(("proj", 0), first_pass)
         for plane in range(2, PACK):
@@ -466,22 +456,18 @@ def tile_flashinferblock_pb_kernel(
 
         gain = keep.tile([P, PLANES], F32, name="gain")
         shift = keep.tile([P, PLANES], F32, name="shift")
-        b_fc1_sb = {}
         fc1_grouped = keep.tile([P, PLANES * N], BF16, name="fc1_grouped", align_bytes=64)
         for c in range(1, CHUNKS):
             grouped["fc1", c] = fc1_grouped
-        steps = [(c, i) for c in range(2) for i in range(TILES - SPAN)]
-        steps.extend([(c, i) for c in range(2) for i in range(TILES - SPAN, TILES)])
-        steps.extend([(c, i) for c in range(2, PAIRED) for i in range(TILES)])
-        steps.extend([(c, i) for i in range(TILES) for c in range(PAIRED, CHUNKS)])
-        issued = [0]
-        last = TILES - 1
+
         for i in range(TILES):
+            span_due = i > SPAN and i % SPAN == 1
+            s = (i - SPAN - 1) // SPAN
             if i > 0:
                 project(i, 0)
             project(i, 1)
             if i == last:
-                issue_matmuls(2)
+                multiply_up_to(2)
             if i + 1 < TILES:
                 residual(i + 1)
             if i + 3 < TILES:
@@ -490,7 +476,12 @@ def tile_flashinferblock_pb_kernel(
                 load_attn(i + 5)
                 load_x(i + 5)
             if i == 3:
-                b_fc1_sb[0] = load_spread("b_fc1_low", b_fc1[: F // 2], F // 2)
+                load_b_fc1(0, "b_fc1_low")
+            if i in (4, 5):
+                load_w_fc1(i - 2, 0)
+                load_w_fc1(i - 2, 1)
+            if i == 6:
+                load_b_fc1(1, "b_fc1_high")
             if i == 0:
                 nc.vector.tensor_copy(out=gain[:], in_=gain_bf16[:])
                 nc.vector.tensor_copy(out=shift[:], in_=shift_bf16[:])
@@ -500,11 +491,9 @@ def tile_flashinferblock_pb_kernel(
             if i + 2 < TILES:
                 quantize_attn(i + 2)
             mean(i)
-            if i >= 3 and i % SPAN == 1:
-                s = (i - 3) // SPAN
+            if span_due:
                 turn_normed(s)
-                for plane in range(PLANES):
-                    gain_shift(s, plane, on_vector=(plane >= PLANES - HOUT_V))
+                gain_and_shift(s, VECTOR_GAINS)
             if i > 0:
                 invert(i - 1)
                 normalise(i - 1)
@@ -513,27 +502,24 @@ def tile_flashinferblock_pb_kernel(
             if i < last:
                 square_sum(i)
                 deviation(i)
+            if span_due:
+                new_grouped(("h", s))
+                interleave(("h", s), both)
+                quantize(("h", s), both)
             if i == 0:
                 interleave(("fc1", 0), second_pass)
                 quantize(("fc1", 0), second_pass)
                 for plane in range(PACK, PLANES):
                     widen(1, plane)
-            if i == 2 and FIRST == 2:
+            if i == 2:
                 interleave(("fc1", 1), first_pass)
                 interleave(("fc1", 1), second_pass)
                 quantize(("fc1", 1), both)
-            if i >= 3 and i % SPAN == 1:
-                new_grouped(("h", s))
-                interleave(("h", s), both)
-                quantize(("h", s), both)
-            if i == 6 and FIRST == 2:
-                for plane in range(EARLY, PLANES):
-                    widen(2, plane)
+            if i == 6:
+                for plane in range(VECTOR_PLANES_FIRST, PLANES):
+                    widen(SHARED, plane)
         for i in range(TILES - 3, TILES):
             store_x_mid(i)
-        b_fc1_sb[1] = load_spread("b_fc1_high", b_fc1[F // 2 :], F // 2)
-        load_w_fc1(2, 0)
-        load_w_fc1(2, 1)
 
         ctx.enter_context(tc.manual_schedule())
         s = last // SPAN
@@ -541,56 +527,51 @@ def tile_flashinferblock_pb_kernel(
         add_bias(0)
         add_bias(1)
         turn_normed(s, range(SPAN - 1))
-        widen(3, THIRD_V)
+        widen(SHARED + 1, VECTOR_PLANES)
         deviation(last)
-        gelu(1)
-        for plane in range(EARLY - 1):
-            widen(2, plane, on_vector=True)
+        gelu_and_store(1)
+        for plane in range(VECTOR_PLANES_FIRST - 1):
+            widen(SHARED, plane, on_vector=True)
         invert(last)
-        issue_matmuls(4)
+        multiply_up_to(4)
         add_bias(2)
         normalise(last)
-        widen(2, EARLY - 1, on_vector=True)
-        interleave_on_gpsimd(("fc1", 2))
-        issue_matmuls(5)
+        widen(SHARED, VECTOR_PLANES_FIRST - 1, on_vector=True)
+        interleave_on_gpsimd(SHARED)
+        multiply_up_to(5)
         turn_normed(s, range(SPAN - 1, SPAN))
         add_bias(3)
-        issue_matmuls(6)
+        multiply_up_to(FIRST_RUN)
         add_bias(4)
-        for plane in range(PLANES):
-            gain_shift(s, plane, on_vector=(plane >= PLANES - TRANS_V))
+        gain_and_shift(s, VECTOR_GAINS_LAST)
+        interleave_on_tensor(SHARED)
         add_bias(5)
-        interleave_on_tensor(("fc1", 2))
-        issue_matmuls(6 + LOOK)
-        gelu(3)
-        for plane in range(THIRD_V + 1, PLANES):
-            widen(3, plane)
-        gelu(5)
-        collect(("fc1", 2))
+        collect(SHARED)
+        multiply_up_to(FIRST_RUN + LOOK)
+        gelu_and_store(3)
+        for plane in range(VECTOR_PLANES + 1, PLANES):
+            widen(SHARED + 1, plane)
+        gelu_and_store(5)
         new_grouped(("h", s))
         interleave(("h", s), both)
-        widen(3, 0, on_vector=True)
+        widen(SHARED + 1, 0, on_vector=True)
         quantize(("h", s), both)
-        issue_matmuls(6 + LOOK)
-        if VECTOR_COLS:
-            interleave_rest(("fc1", 2))
-        for plane in range(1, THIRD_V):
-            widen(3, plane, on_vector=True)
-        quantize(("fc1", 2), both)
-        interleave_on_gpsimd(("fc1", 3))
+        interleave_rest(SHARED)
+        widen(SHARED + 1, 1, on_vector=True)
+        quantize(("fc1", SHARED), both)
+        interleave_on_gpsimd(SHARED + 1)
         for plane in range(VECTOR_PLANES, PLANES):
-            widen(4, plane)
-        interleave_on_tensor(("fc1", 3))
-        load_w_fc1(3, 0)
-        load_w_fc1(3, 1)
+            widen(SHARED + 2, plane)
+        interleave_on_tensor(SHARED + 1)
 
-        for n in range(6, len(steps)):
-            window, place = divmod(n, TILES)
+        for n in range(FIRST_RUN, len(steps)):
+            run, place = divmod(n - FIRST_RUN, TILES)
+            coming = SHARED + 1 + run
             add_bias(n)
-            gelu(n)
-            if n >= PLACE + LAG and (n - PLACE - LAG) % TILES == 0 and (n - PLACE - LAG) // TILES + 3 < CHUNKS:
-                collect(("fc1", (n - PLACE - LAG) // TILES + 3))
-            issue_matmuls(n + 1 + LOOK)
-            if place == PLACE and window > 0 and window + 2 < CHUNKS:
-                prepare(window + 2)
-                issue_matmuls(n + 1 + LOOK)
+            gelu_and_store(n)
+            if place == 1 and coming < CHUNKS:
+                collect(coming)
+            multiply_up_to(n + 1 + LOOK)
+            if place == TILES - 1 and coming < CHUNKS:
+                finish_chunk(coming)
+                multiply_up_to(n + 1 + LOOK)

from contextlib import ExitStack

import concourse.mybir as mybir
from concourse.masks import make_identity

T, D, F = 1024, 1024, 4096
EPS = 1e-5
FLOPS = 2 * T * D * (D + F)
BYTES = 2 * T * D * 2 + D * D * 2 + D * F + D * 4 + (3 * D + F) * 2 + T * D * 4 + T * F * 4

F32 = mybir.dt.float32
BF16 = mybir.dt.bfloat16
U32 = mybir.dt.uint32
U8 = mybir.dt.uint8
FP8 = mybir.dt.float8_e4m3fn
FP8X4 = mybir.dt.float8_e4m3fn_x4
ALU = mybir.AluOpType
ACT = mybir.ActivationFunctionType

P = 128
PACK = 4
PASSES = D // (P * PACK)
PLANES = PASSES * PACK
N = 512
TILES = T // P
CHUNKS = F // N
BLOCK = 2 * N
SPAN = 2
PAIRED = CHUNKS - 2
SHARED = 2
RUN = 4

GPSIMD_COLS = 704
TENSOR_COLS = 256
VECTOR_PLANES = 2
VECTOR_PLANES_FIRST = 3
VECTOR_GAINS = 2
VECTOR_GAINS_LAST = 6

FIRST_RUN = TILES - SPAN
LOOK = 6
CODE_BUFS = {"proj": 2, "h": TILES // SPAN, "fc1": 3}
ROW_BUFS = 16
WIDE_BUFS = 13


def tile_flashinferblock_pb_kernel(
    tc, attn_out, x, w_proj, b_proj, g2, beta2, w_fc1_bytes, w_fc1_scale, b_fc1, out_0, out_1
):
    nc = tc.nc
    attn_rows = attn_out.rearrange("b s d -> (b s) d")
    x_rows = x.rearrange("b s d -> (b s) d")
    x_mid_rows = out_0.rearrange("b s d -> (b s) d")
    hid_rows = out_1.rearrange("b s f -> (b s) f")
    w_proj_k = w_proj.rearrange("(g p t) n -> g p t n", p=P, t=PACK)
    w_fc1_k = w_fc1_bytes.rearrange("(g p t) n -> g p t n", p=P, t=PACK)

    with ExitStack() as ctx:
        keep = ctx.enter_context(tc.tile_pool(name="keep", bufs=1))
        work = ctx.enter_context(tc.tile_pool(name="work", bufs=2))
        psum = ctx.enter_context(tc.psum_pool(name="psum", bufs=8))
        ctx.enter_context(tc.manual_schedule(engines={mybir.EngineType.SP, mybir.EngineType.PE}))

        planes, grouped, codes, scales = {}, {}, {}, {}
        attn_sb, x_sb, w_bytes, attn_grouped, attn_codes, attn_scales = {}, {}, {}, {}, {}, {}
        resid, acc, x_mid, sums, neg_mean, sq_sum, std, rstd, normed, staged = {}, {}, {}, {}, {}, {}, {}, {}, {}, {}
        b_fc1_sb = {}
        first_pass, second_pass, both = slice(0, 1), slice(1, 2), slice(0, 2)
        last = TILES - 1

        steps = [(c, i) for c in range(SHARED) for i in range(TILES - SPAN)]
        steps.extend([(c, i) for c in range(SHARED) for i in range(TILES - SPAN, TILES)])
        steps.extend([(c, i) for c in range(SHARED, PAIRED) for i in range(TILES)])
        steps.extend([(c, i) for i in range(TILES) for c in range(PAIRED, CHUNKS)])
        multiplied = []

        def rows(i):
            return slice(i * P, (i + 1) * P)

        def cols(j):
            return slice(j * N, (j + 1) * N)

        def new_bank():
            return psum.tile([P, N], F32, name="bank")

        def width(key):
            return SPAN * P if key[0] == "h" else N

        def new_planes(key):
            name, bufs = ("h_planes", 2) if key[0] == "h" else ("planes", 4)
            planes[key] = work.tile([P, PLANES * width(key)], BF16, name=name, bufs=bufs, align_bytes=64)

        def new_grouped(key):
            grouped[key] = work.tile([P, PLANES * width(key)], BF16, name="grouped", bufs=2, align_bytes=64)

        def load_w_proj(half, g):
            if g == 0:
                new_planes(("proj", half))
            nc.sync.dma_start(
                out=planes["proj", half][:].rearrange("p (g t n) -> p g t n", g=PASSES, t=PACK)[:, g],
                in_=w_proj_k[g][:, :, cols(half)],
            )

        def load_attn(i):
            attn_sb[i] = work.tile([P, D], BF16, name="attn_sb", tag="rows", bufs=ROW_BUFS)
            nc.sync.dma_start(out=attn_sb[i][:], in_=attn_rows[rows(i), :])

        def load_x(i):
            x_sb[i] = work.tile([P, D], BF16, name="x_sb", tag="rows", bufs=ROW_BUFS)
            nc.sync.dma_start(out=x_sb[i][:], in_=x_rows[rows(i), :])

        def load_w_fc1(b, g, slots=slice(0, PACK)):
            if slots.start == 0:
                w_bytes[b, g] = work.tile([P, PACK * BLOCK], U8, name="w_bytes", bufs=6)
            nc.sync.dma_start(
                out=w_bytes[b, g][:].rearrange("p (t n) -> p t n", t=PACK)[:, slots],
                in_=w_fc1_k[g][:, slots, b * BLOCK : (b + 1) * BLOCK],
            )

        def load_columns(name, vector, dtype):
            tile = keep.tile([P, PLANES], dtype, name=name)
            nc.scalar.dma_start(
                out=tile[:].rearrange("p (g t) -> p g t", t=PACK),
                in_=vector.rearrange("(g p t) -> p g t", p=P, t=PACK),
            )
            return tile

        def load_b_fc1(half, name):
            b_fc1_sb[half] = keep.tile([P, F // 2], BF16, name=name)
            nc.sync.dma_start(
                out=b_fc1_sb[half][:], in_=b_fc1[half * (F // 2) : (half + 1) * (F // 2)].partition_broadcast(P)
            )

        def widen(c, plane, on_vector=False):
            g, t = divmod(plane, PACK)
            if ("fc1", c) not in planes:
                new_planes(("fc1", c))
            b, first = divmod(c * N, BLOCK)
            source = w_bytes[b, g][:, t * BLOCK + first : t * BLOCK + first + N].bitcast(FP8)
            scale = w_scale[:, plane : plane + 1]
            target = planes["fc1", c][:, cols(plane if c < SHARED else t * PASSES + g)]
            if on_vector:
                nc.vector.tensor_scalar(out=target, in0=source, scalar1=scale, scalar2=None, op0=ALU.mult)
            else:
                nc.scalar.activation(out=target, in_=source, func=ACT.Copy, scale=scale)

        def interleave(key, passes):
            nc.vector.tensor_copy(
                out=grouped[key][:].rearrange("p (g c i t) -> p g c t i", g=PASSES, i=RUN, t=PACK)[:, passes],
                in_=planes[key][:].rearrange("p (g t c i) -> p g c t i", g=PASSES, i=RUN, t=PACK)[:, passes],
            )

        def interleave_on_gpsimd(c):
            nc.gpsimd.tensor_scalar(
                out=fc1_grouped[:].rearrange("p (q t) -> p q t", t=PACK)[:, :GPSIMD_COLS],
                in0=planes["fc1", c][:].rearrange("p (t q) -> p q t", t=PACK)[:, :GPSIMD_COLS],
                scalar1=1.0,
                scalar2=0.0,
                op0=ALU.mult,
                op1=ALU.add,
            )

        def interleave_on_tensor(c):
            source = planes["fc1", c][:].rearrange("p (t q) -> p q t", t=PACK)
            acc["interleaved", c] = psum.tile([P, PACK * TENSOR_COLS], BF16, name="bank")
            for q in range(0, TENSOR_COLS, P):
                nc.tensor.matmul(
                    acc["interleaved", c][:, PACK * q : PACK * (q + P)],
                    lhsT=ident_bf16[:],
                    rhs=source[:, GPSIMD_COLS + q : GPSIMD_COLS + q + P],
                    start=True,
                    stop=True,
                )

        def collect(c):
            nc.vector.tensor_copy(
                out=fc1_grouped[:, PACK * GPSIMD_COLS : PACK * (GPSIMD_COLS + TENSOR_COLS)],
                in_=acc["interleaved", c][:],
            )

        def interleave_rest(c):
            first = (GPSIMD_COLS + TENSOR_COLS) // RUN
            nc.vector.tensor_copy(
                out=fc1_grouped[:].rearrange("p (c i t) -> p c t i", i=RUN, t=PACK)[:, first:],
                in_=planes["fc1", c][:].rearrange("p (t c i) -> p c t i", i=RUN, t=PACK)[:, first:],
            )

        def quantize(key, passes):
            kind = key[0]
            if passes.start == 0:
                shape = [P, PASSES * width(key)]
                codes[key] = work.tile(shape, U32, name=kind + "_codes", bufs=CODE_BUFS[kind], align_bytes=64)
                scales[key] = work.tile(shape, U8, name=kind + "_scales", bufs=CODE_BUFS[kind], align_bytes=64)
            words = slice(passes.start * width(key), passes.stop * width(key))
            nc.vector.quantize_mx(
                out=codes[key][:, words].bitcast(FP8X4),
                scales=scales[key][:, words],
                in_=grouped[key][:, PACK * words.start : PACK * words.stop],
            )

        def turn_attn(i):
            words = attn_sb[i][:].bitcast(F32)
            bank = new_bank()
            for g in range(PASSES):
                for u in range(2):
                    j = 2 * g + u
                    nc.tensor.transpose(
                        bank[:, j * P : (j + 1) * P], words[:, 2 * P * g + u : 2 * P * (g + 1) : 2], ident_f32[:]
                    )
            attn_grouped[i] = work.tile([P, D], BF16, name="attn_grouped", bufs=3, align_bytes=64)
            nc.scalar.copy(
                out=attn_grouped[i][:].bitcast(F32).rearrange("p (g r u) -> p g r u", g=PASSES, u=2),
                in_=bank[:].rearrange("p (g u r) -> p g r u", g=PASSES, u=2),
            )

        def quantize_attn(i):
            attn_codes[i] = work.tile([P, PASSES * P], U32, name="attn_codes", bufs=3, align_bytes=64)
            attn_scales[i] = work.tile([P, PASSES * P], U8, name="attn_scales", bufs=3, align_bytes=64)
            nc.vector.quantize_mx(
                out=attn_codes[i][:].bitcast(FP8X4), scales=attn_scales[i][:], in_=attn_grouped[i][:]
            )

        def residual(i):
            for half in range(2):
                bank = new_bank()
                nc.tensor.matmul(bank[:], lhsT=ident_bf16[:], rhs=x_sb[i][:, cols(half)], start=True, stop=False)
                nc.tensor.matmul(bank[:], lhsT=ones[:], rhs=b_proj_row[:, cols(half)], start=False, stop=True)
                resid[i, half] = work.tile([P, N], F32, name="staged", tag="rows", bufs=ROW_BUFS)
                nc.scalar.copy(out=resid[i, half][:], in_=bank[:])

        def project(i, half):
            acc["proj", i, half] = new_bank()
            for g in range(PASSES):
                nc.tensor.matmul_mx(
                    out=acc["proj", i, half][:],
                    lhsT=attn_codes[i][:, g * P : (g + 1) * P].bitcast(FP8X4),
                    lhsT_scale=attn_scales[i][:, g * P : (g + 1) * P],
                    rhs=codes["proj", half][:, cols(g)].bitcast(FP8X4),
                    rhs_scale=scales["proj", half][:, cols(g)],
                    start=(g == 0),
                    stop=(g == PASSES - 1),
                )

        def add_residual(i, half):
            if half == 0:
                x_mid[i] = work.tile([P, D], F32, name="x_mid", tag="wide", bufs=WIDE_BUFS)
                sums[i] = work.tile([P, 2], F32, name="sums")
            nc.vector.scalar_tensor_tensor(
                out=x_mid[i][:, cols(half)],
                in0=acc["proj", i, half][:],
                scalar=1.0,
                in1=resid[i, half][:],
                op0=ALU.mult,
                op1=ALU.add,
                accum_out=sums[i][:, half : half + 1],
            )

        def store_x_mid(i):
            nc.sync.dma_start(out=x_mid_rows[rows(i), :], in_=x_mid[i][:])

        def mean(i):
            neg_mean[i] = work.tile([P, 1], F32, name="neg_mean", bufs=3)
            nc.vector.tensor_scalar(
                out=neg_mean[i][:],
                in0=sums[i][:, 0:1],
                scalar1=sums[i][:, 1:2],
                scalar2=-1.0 / D,
                op0=ALU.add,
                op1=ALU.mult,
            )

        def square_sum(i):
            sq_sum[i] = work.tile([P, 1], F32, name="sq_sum")
            squares = work.tile([P, D], BF16, name="squares", bufs=1)
            nc.scalar.activation(
                out=squares[:], in_=x_mid[i][:], func=ACT.Square, bias=neg_mean[i][:], accum_out=sq_sum[i][:]
            )

        def deviation(i):
            std[i] = work.tile([P, 1], F32, name="std")
            nc.scalar.activation(out=std[i][:], in_=sq_sum[i][:], func=ACT.Sqrt, scale=1.0 / D, bias=EPS)

        def invert(i):
            rstd[i] = work.tile([P, 1], F32, name="rstd")
            nc.vector.reciprocal(out=rstd[i][:], in_=std[i][:])

        def normalise(i):
            normed[i] = work.tile([P, D], F32, name="normed", tag="wide", bufs=WIDE_BUFS)
            nc.vector.tensor_scalar(
                out=normed[i][:].rearrange("r (t q) -> r q t", t=PACK),
                in0=x_mid[i][:].rearrange("r (q t) -> r q t", t=PACK),
                scalar1=neg_mean[i][:],
                scalar2=rstd[i][:],
                op0=ALU.add,
                op1=ALU.mult,
            )

        def turn_normed(s, tiles=range(SPAN)):
            for j in tiles:
                for plane in range(PLANES):
                    g, t = divmod(plane, PACK)
                    if j == 0 and plane % 2 == 0:
                        acc["h", s, plane // 2] = new_bank()
                    first = (t * PASSES + g) * P
                    column = (plane % 2 * SPAN + j) * P
                    nc.tensor.transpose(
                        acc["h", s, plane // 2][:, column : column + P],
                        normed[s * SPAN + j][:, first : first + P],
                        ident_f32[:],
                    )

        def gain_and_shift(s, on_vector):
            new_planes(("h", s))
            for plane in range(PLANES):
                source = acc["h", s, plane // 2][:, plane % 2 * SPAN * P : (plane % 2 + 1) * SPAN * P]
                target = planes["h", s][:, plane * SPAN * P : (plane + 1) * SPAN * P]
                if plane >= PLANES - on_vector:
                    nc.vector.tensor_scalar(
                        out=target,
                        in0=source,
                        scalar1=gain[:, plane : plane + 1],
                        scalar2=shift[:, plane : plane + 1],
                        op0=ALU.mult,
                        op1=ALU.add,
                    )
                else:
                    nc.scalar.activation(
                        out=target,
                        in_=source,
                        func=ACT.Identity,
                        scale=gain[:, plane : plane + 1],
                        bias=shift[:, plane : plane + 1],
                    )

        def multiply_up_to(stop):
            while len(multiplied) < min(stop, len(steps)):
                c, i = steps[len(multiplied)]
                s, j = divmod(i, SPAN)
                if ("fc1", c) not in codes or ("h", s) not in codes:
                    return
                bank = new_bank()
                for g in range(PASSES):
                    nc.tensor.matmul_mx(
                        out=bank[:],
                        lhsT=codes["h", s][:, (g * SPAN + j) * P : (g * SPAN + j + 1) * P].bitcast(FP8X4),
                        lhsT_scale=scales["h", s][:, (g * SPAN + j) * P : (g * SPAN + j + 1) * P],
                        rhs=codes["fc1", c][:, cols(g)].bitcast(FP8X4),
                        rhs_scale=scales["fc1", c][:, cols(g)],
                        start=(g == 0),
                        stop=(g == PASSES - 1),
                    )
                multiplied.append(bank)

        def add_bias(n):
            if n % 2 == 0:
                staged[n // 2] = work.tile([P, 2 * N], F32, name="staged_pair", tag="wide", bufs=WIDE_BUFS)
            half, first = divmod(steps[n][0] * N, F // 2)
            nc.vector.tensor_tensor(
                out=staged[n // 2][:, cols(n % 2)],
                in0=multiplied[n][:],
                in1=b_fc1_sb[half][:, first : first + N],
                op=ALU.add,
            )

        def gelu_and_store(n):
            c, i = steps[n]
            if n + 2 >= len(steps):
                tile = staged[n // 2][:, cols(n % 2)]
                nc.scalar.activation(out=tile, in_=tile, func=ACT.Gelu)
                nc.sync.dma_start(out=hid_rows[rows(i), cols(c)], in_=tile)
            elif n % 2:
                tile = staged[n // 2][:]
                nc.scalar.activation(out=tile, in_=tile, func=ACT.Gelu)
                if c < PAIRED:
                    nc.sync.dma_start(
                        out=hid_rows[(i - 1) * P : (i + 1) * P, cols(c)].rearrange("(j p) f -> p j f", p=P),
                        in_=tile.rearrange("p (j f) -> p j f", j=2),
                    )
                else:
                    nc.sync.dma_start(out=hid_rows[rows(i), PAIRED * N :], in_=tile)

        def finish_chunk(c):
            interleave_rest(c)
            if c + 1 < CHUNKS:
                for plane in range(VECTOR_PLANES):
                    widen(c + 1, plane, on_vector=True)
            quantize(("fc1", c), both)
            if c + 1 < CHUNKS:
                interleave_on_gpsimd(c + 1)
            if c + 2 < CHUNKS:
                for plane in range(VECTOR_PLANES, PLANES):
                    widen(c + 2, plane)
            if c + 1 < CHUNKS:
                interleave_on_tensor(c + 1)

        b_proj_row = keep.tile([P, D], BF16, name="b_proj_row")
        nc.vector.memset(b_proj_row[:], 0.0)
        ones = keep.tile([P, P], BF16, name="ones")
        nc.vector.memset(ones[:], 1.0)
        w_scale = load_columns("w_scale", w_fc1_scale.rearrange("k o -> (k o)"), F32)
        gain_bf16 = load_columns("gain_bf16", g2, BF16)
        shift_bf16 = load_columns("shift_bf16", beta2, BF16)
        nc.scalar.dma_start(out=b_proj_row[0:1, :], in_=b_proj.rearrange("(o d) -> o d", o=1))
        load_w_fc1(0, 0, slice(0, 2))
        load_w_proj(0, 0)
        load_w_fc1(0, 0, slice(2, PACK))
        load_w_proj(0, 1)
        load_attn(0)
        load_w_fc1(0, 1)
        load_w_proj(1, 0)
        load_x(0)
        load_w_proj(1, 1)
        for i in range(1, 5):
            load_attn(i)
            load_x(i)
        load_w_fc1(1, 0)
        load_w_fc1(1, 1)

        nc.scalar.activation(out=ones[:], in_=ones[:], func=ACT.Sqrt)
        ident_f32 = keep.tile([P, P], F32, name="ident_f32")
        make_identity(nc, ident_f32[:])
        ident_bf16 = keep.tile([P, P], BF16, name="ident_bf16")
        make_identity(nc, ident_bf16[:])

        widen(0, 0)
        widen(1, 0, on_vector=True)
        widen(1, 1, on_vector=True)
        widen(0, 1)
        new_grouped(("proj", 0))
        interleave(("proj", 0), first_pass)
        for plane in range(2, PACK):
            widen(0, plane)
        turn_attn(0)
        quantize(("proj", 0), first_pass)
        interleave(("proj", 0), second_pass)
        for plane in range(2, PACK):
            widen(1, plane)
        new_grouped(("fc1", 0))
        interleave(("fc1", 0), first_pass)
        quantize(("proj", 0), second_pass)
        quantize_attn(0)
        new_grouped(("proj", 1))
        interleave(("proj", 1), first_pass)
        quantize(("fc1", 0), first_pass)
        residual(0)
        project(0, 0)
        quantize(("proj", 1), first_pass)
        for plane in range(PACK, PLANES):
            widen(0, plane)
        turn_attn(1)
        interleave(("proj", 1), second_pass)
        add_residual(0, 0)
        quantize(("proj", 1), second_pass)
        quantize_attn(1)
        turn_attn(2)

        gain = keep.tile([P, PLANES], F32, name="gain")
        shift = keep.tile([P, PLANES], F32, name="shift")
        fc1_grouped = keep.tile([P, PLANES * N], BF16, name="fc1_grouped", align_bytes=64)
        for c in range(1, CHUNKS):
            grouped["fc1", c] = fc1_grouped

        for i in range(TILES):
            span_due = i > SPAN and i % SPAN == 1
            s = (i - SPAN - 1) // SPAN
            if i > 0:
                project(i, 0)
            project(i, 1)
            if i == last:
                multiply_up_to(2)
            if i + 1 < TILES:
                residual(i + 1)
            if i + 3 < TILES:
                turn_attn(i + 3)
            if i + 5 < TILES:
                load_attn(i + 5)
                load_x(i + 5)
            if i == 3:
                load_b_fc1(0, "b_fc1_low")
            if i in (4, 5):
                load_w_fc1(i - 2, 0)
                load_w_fc1(i - 2, 1)
            if i == 6:
                load_b_fc1(1, "b_fc1_high")
            if i == 0:
                nc.vector.tensor_copy(out=gain[:], in_=gain_bf16[:])
                nc.vector.tensor_copy(out=shift[:], in_=shift_bf16[:])
            if i > 0:
                add_residual(i, 0)
            add_residual(i, 1)
            if i + 2 < TILES:
                quantize_attn(i + 2)
            mean(i)
            if span_due:
                turn_normed(s)
                gain_and_shift(s, VECTOR_GAINS)
            if i > 0:
                invert(i - 1)
                normalise(i - 1)
            if i >= 3:
                store_x_mid(i - 3)
            if i < last:
                square_sum(i)
                deviation(i)
            if span_due:
                new_grouped(("h", s))
                interleave(("h", s), both)
                quantize(("h", s), both)
            if i == 0:
                interleave(("fc1", 0), second_pass)
                quantize(("fc1", 0), second_pass)
                for plane in range(PACK, PLANES):
                    widen(1, plane)
            if i == 2:
                interleave(("fc1", 1), first_pass)
                interleave(("fc1", 1), second_pass)
                quantize(("fc1", 1), both)
            if i == 6:
                for plane in range(VECTOR_PLANES_FIRST, PLANES):
                    widen(SHARED, plane)
        for i in range(TILES - 3, TILES):
            store_x_mid(i)

        ctx.enter_context(tc.manual_schedule())
        s = last // SPAN
        square_sum(last)
        add_bias(0)
        add_bias(1)
        turn_normed(s, range(SPAN - 1))
        widen(SHARED + 1, VECTOR_PLANES)
        deviation(last)
        gelu_and_store(1)
        for plane in range(VECTOR_PLANES_FIRST - 1):
            widen(SHARED, plane, on_vector=True)
        invert(last)
        multiply_up_to(4)
        add_bias(2)
        normalise(last)
        widen(SHARED, VECTOR_PLANES_FIRST - 1, on_vector=True)
        interleave_on_gpsimd(SHARED)
        multiply_up_to(5)
        turn_normed(s, range(SPAN - 1, SPAN))
        add_bias(3)
        multiply_up_to(FIRST_RUN)
        add_bias(4)
        gain_and_shift(s, VECTOR_GAINS_LAST)
        interleave_on_tensor(SHARED)
        add_bias(5)
        collect(SHARED)
        multiply_up_to(FIRST_RUN + LOOK)
        gelu_and_store(3)
        for plane in range(VECTOR_PLANES + 1, PLANES):
            widen(SHARED + 1, plane)
        gelu_and_store(5)
        new_grouped(("h", s))
        interleave(("h", s), both)
        widen(SHARED + 1, 0, on_vector=True)
        quantize(("h", s), both)
        interleave_rest(SHARED)
        widen(SHARED + 1, 1, on_vector=True)
        quantize(("fc1", SHARED), both)
        interleave_on_gpsimd(SHARED + 1)
        for plane in range(VECTOR_PLANES, PLANES):
            widen(SHARED + 2, plane)
        interleave_on_tensor(SHARED + 1)

        for n in range(FIRST_RUN, len(steps)):
            run, place = divmod(n - FIRST_RUN, TILES)
            coming = SHARED + 1 + run
            add_bias(n)
            gelu_and_store(n)
            if place == 1 and coming < CHUNKS:
                collect(coming)
            multiply_up_to(n + 1 + LOOK)
            if place == TILES - 1 and coming < CHUNKS:
                finish_chunk(coming)
                multiply_up_to(n + 1 + LOOK)
